import numpy as np
import ml_dtypes


def mxq(x, axis, fmt="e4m3"):
    dtype, down = {"e4m3": (ml_dtypes.float8_e4m3fn, 7), "e5m2": (ml_dtypes.float8_e5m2, 14)}[fmt]
    v = np.moveaxis(np.asarray(x, np.float32).astype(ml_dtypes.bfloat16).astype(np.float64), axis, -1)
    blocks = v.reshape(v.shape[:-1] + (-1, 32))
    amax = np.abs(blocks).max(-1, keepdims=True)
    byte = np.maximum(np.where(amax > 0, np.frexp(amax)[1] - 1 + 127, 0) - down, 1)
    scale = np.exp2(byte - 127.0)
    codes = (blocks / scale).astype(np.float32).astype(dtype).astype(np.float64)
    return np.moveaxis((codes * scale).reshape(v.shape), -1, axis)


WIDE = False


def mx_kscale(k):
    if not WIDE:
        return np.ones(k)
    levels = np.array([10, -10, 5, -5, 0])
    a = np.random.permutation(np.resize(levels, k // 512 * 4)).reshape(k // 512, 4)
    idx = np.arange(k)
    return np.exp2(a[idx // 512, idx % 128 // 32])


BF16 = ml_dtypes.bfloat16


def bf(x):
    return np.asarray(x, np.float32).astype(BF16)


def f64(x):
    return np.asarray(x).astype(np.float64)


B, I, H, Q = 256, 512, 512, 4

HAM = (((0, 1.0), (1, 1.0), (2, 1.0), (3, 1.0)),
       ((1, -1.0), (0, 1.0), (3, 1.0), (2, -1.0)),
       ((2, -1.0), (3, -1.0), (0, 1.0), (1, 1.0)),
       ((3, -1.0), (2, 1.0), (1, -1.0), (0, 1.0)))


def sigmoid(v):
    return 1.0 / (1.0 + np.exp(-v))


def qcomp(vq, Wq, d):
    return sum(HAM[a][d][1] * (vq[:, :, a] @ Wq[HAM[a][d][0]].T) for a in range(Q))


def setup_inputs():
    s, t = mx_kscale(I), mx_kscale(H)
    ws, us = 0.9 / np.sqrt(Q * I), 0.9 / np.sqrt(Q * H)
    return {"x": bf(np.random.standard_normal((B, I, Q)) * s[None, :, None]),
            "h": bf(np.random.standard_normal((B, H, Q)) * t[None, :, None]),
            "c": bf(np.random.standard_normal((B, H, Q))),
            "Wi_w": bf(np.random.standard_normal((Q, H, I)) * ws / s),
            "Wf_w": bf(np.random.standard_normal((Q, H, I)) * ws / s),
            "Wo_w": bf(np.random.standard_normal((Q, H, I)) * ws / s),
            "Wc_w": bf(np.random.standard_normal((Q, H, I)) * ws / s),
            "Ui_w": bf(np.random.standard_normal((Q, H, H)) * us / t),
            "Uf_w": bf(np.random.standard_normal((Q, H, H)) * us / t),
            "Uo_w": bf(np.random.standard_normal((Q, H, H)) * us / t),
            "Uc_w": bf(np.random.standard_normal((Q, H, H)) * us / t),
            "Ui_br": bf(np.random.standard_normal(H) * 0.5),
            "Uf_br": bf(np.random.standard_normal(H) * 0.5),
            "Uo_br": bf(np.random.standard_normal(H) * 0.5),
            "Uc_b": bf(np.random.standard_normal((H, Q)) * 0.5)}


def reference(x, h, c, Wi_w, Wf_w, Wo_w, Wc_w, Ui_w, Uf_w, Uo_w, Uc_w, Ui_br, Uf_br, Uo_br, Uc_b):
    xq = mxq(f64(x), 1, "e4m3")
    hq = mxq(f64(h), 1, "e4m3")
    i = sigmoid(qcomp(xq, mxq(f64(Wi_w), 2, "e4m3"), 0) + qcomp(hq, mxq(f64(Ui_w), 2, "e4m3"), 0) + f64(Ui_br))[..., None]
    f = sigmoid(qcomp(xq, mxq(f64(Wf_w), 2, "e4m3"), 0) + qcomp(hq, mxq(f64(Uf_w), 2, "e4m3"), 0) + f64(Uf_br))[..., None]
    o = sigmoid(qcomp(xq, mxq(f64(Wo_w), 2, "e4m3"), 0) + qcomp(hq, mxq(f64(Uo_w), 2, "e4m3"), 0) + f64(Uo_br))[..., None]
    wc = mxq(f64(Wc_w), 2, "e4m3")
    uc = mxq(f64(Uc_w), 2, "e4m3")
    p = np.stack([qcomp(xq, wc, d) + qcomp(hq, uc, d) for d in range(Q)], axis=-1)
    c_tilde = np.tanh(p + f64(Uc_b))
    c_t = f * f64(c) + i * c_tilde
    h_t = o * np.tanh(c_t)
    return h_t, c_t

@@ -1,0 +1,340 @@
+from contextlib import ExitStack
+
+import concourse.mybir as mybir
+from concourse.masks import make_identity
+
+F32 = mybir.dt.float32
+BF16 = mybir.dt.bfloat16
+U32 = mybir.dt.uint32
+U8 = mybir.dt.uint8
+FP8X4 = mybir.dt.float8_e4m3fn_x4
+ACT = mybir.ActivationFunctionType
+ALU = mybir.AluOpType
+
+P = 128
+PACK = 4
+BATCH, FEAT, OUT, Q = 256, 512, 512, 4
+BT = BATCH // P
+WORDS = FEAT // 2
+HALVES = WORDS // P
+ROWS = OUT // P
+BANK = 512
+UNIT = 2
+PARTS = 2 * Q // UNIT
+VERSIONS = 2 * Q - 1
+CHUNK = BANK // Q
+LEAD = 2
+
+HAM = (
+    ((0, 1.0), (1, 1.0), (2, 1.0), (3, 1.0)),
+    ((1, -1.0), (0, 1.0), (3, 1.0), (2, -1.0)),
+    ((2, -1.0), (3, -1.0), (0, 1.0), (1, 1.0)),
+    ((3, -1.0), (2, 1.0), (1, -1.0), (0, 1.0)),
+)
+
+FLOPS = 2 * BATCH * FEAT * OUT * 2 * (3 * Q + Q * Q)
+
+CAND, F_GATE, I_GATE, O_GATE = 0, 1, 2, 3
+
+
+def input_version(d, w_comp):
+    a = [a for a in range(Q) if HAM[a][d][0] == w_comp][0]
+    return a if HAM[a][d][1] > 0 else Q - 1 + a
+
+
+def tile_quaternionlstmcell_pa_kernel(
+    tc, x, h, c, Wi_w, Wf_w, Wo_w, Wc_w, Ui_w, Uf_w, Uo_w, Uc_w, Ui_br, Uf_br, Uo_br, Uc_b, out_0, out_1
+):
+    nc = tc.nc
+    weights = {CAND: (Wc_w, Uc_w), F_GATE: (Wf_w, Uf_w), I_GATE: (Wi_w, Ui_w), O_GATE: (Wo_w, Uo_w)}
+    gate_bias = {F_GATE: Uf_br, I_GATE: Ui_br, O_GATE: Uo_br}
+    n_units = len(weights) * PARTS
+    h_rows = out_0.rearrange("(p t) m a -> p t (m a)", t=BT)
+    c_rows = out_1.rearrange("(p t) m a -> p t (m a)", t=BT)
+
+    with ExitStack() as stack:
+        stack.enter_context(tc.manual_schedule())
+        keep = stack.enter_context(tc.tile_pool(name="keep", bufs=1))
+        raw_pool = stack.enter_context(tc.tile_pool(name="raw", bufs=5))
+        grouped_pool = stack.enter_context(tc.tile_pool(name="grouped", bufs=3))
+        gate_q_pool = stack.enter_context(tc.tile_pool(name="gate_q", bufs=7))
+        cand_q_pool = stack.enter_context(tc.tile_pool(name="cand_q", bufs=PARTS))
+        flip_pool = stack.enter_context(tc.psum_pool(name="flip", bufs=4))
+        acc_pool = stack.enter_context(tc.psum_pool(name="acc", bufs=4))
+
+        ident = keep.tile([P, P], F32)
+        make_identity(nc, ident[:])
+        warm = keep.tile([P, 1], F32)
+        nc.vector.memset(warm[:], 0.0)
+        nc.scalar.activation(out=warm[:], in_=warm[:], func=ACT.Sigmoid)
+
+        bias = {}
+        c_raw = keep.tile([P, BT, OUT * Q], BF16)
+        act_raw = {}
+        act_codes = {}
+        act_scales = {}
+        raw_units = []
+        grouped_units = {}
+        unit_codes = {}
+        unit_scales = {}
+
+        def transpose_unit(u):
+            raw_words = raw_units[u][:].bitcast(F32)
+            grouped = grouped_pool.tile([P, UNIT, OUT, PACK], BF16, name="grouped_unit", tag="grouped_unit", align_bytes=64)
+            grouped_words = grouped[:].bitcast(F32)
+            for comp in range(UNIT):
+                for j0 in range(0, ROWS, 2):
+                    flipped = flip_pool.tile([P, BANK], F32, name="flipped", tag="flip")
+                    for j in range(2):
+                        for u2 in range(HALVES):
+                            block = HALVES * j + u2
+                            nc.tensor.transpose(
+                                flipped[:, block * P : (block + 1) * P],
+                                raw_words[:, comp, j0 + j, u2 * P : (u2 + 1) * P],
+                                ident[:],
+                            )
+                    nc.scalar.copy(
+                        out=grouped_words[:, comp].rearrange("p (q g j) u -> p g q j u", g=ROWS // 2, j=2)[:, j0 // 2],
+                        in_=flipped[:].rearrange("p (j u q) -> p q j u", j=2, u=HALVES),
+                    )
+            grouped_units[u] = grouped
+
+        def quantise_unit(u):
+            pool = cand_q_pool if u // PARTS == CAND else gate_q_pool
+            codes = pool.tile([P, UNIT, OUT], U32, name="unit_codes", tag="unit_codes", align_bytes=64)
+            scales = pool.tile([P, UNIT, OUT], U8, name="unit_scales", tag="unit_scales", align_bytes=64)
+            nc.vector.quantize_mx(
+                out=codes[:].rearrange("p c m -> p (c m)").bitcast(FP8X4),
+                scales=scales[:].rearrange("p c m -> p (c m)"),
+                in_=grouped_units[u][:].rearrange("p c m k -> p (c m k)"),
+            )
+            unit_codes[u] = codes
+            unit_scales[u] = scales
+
+        def multiply(acc, d, bt, u, comp, cols):
+            part = u % PARTS
+            name = "x" if part < PARTS // 2 else "h"
+            version = input_version(d, UNIT * (part % (PARTS // 2)) + comp)
+            m0, width = cols
+            nc.tensor.matmul_mx(
+                out=acc,
+                lhsT=act_codes[name][:, version, bt, :].bitcast(FP8X4),
+                lhsT_scale=act_scales[name][:, version, bt, :],
+                rhs=unit_codes[u][:, comp, m0 : m0 + width].bitcast(FP8X4),
+                rhs_scale=unit_scales[u][:, comp, m0 : m0 + width],
+                start=(part == 0 and comp == 0),
+                stop=(part == PARTS - 1 and comp == UNIT - 1),
+            )
+
+        def new_acc():
+            acc = acc_pool.tile([P, BANK], F32, name="acc", tag="acc")
+            return acc
+
+        whole = (0, OUT)
+        halves = ((0, OUT // 2), (OUT // 2, OUT // 2))
+
+        with tc.tile_pool(name="prep", bufs=1) as prep:
+            def load_input(name, v):
+                act_raw[name] = prep.tile([P, BT, FEAT * Q], BF16, name="raw_" + name)
+                nc.sync.dma_start(out=act_raw[name][:], in_=v.rearrange("(p t) n a -> p t (n a)", t=BT))
+
+            load_input("x", x)
+            for u in range(n_units):
+                if u == PARTS // 2:
+                    load_input("h", h)
+                if u == PARTS + PARTS // 2:
+                    bias[CAND] = keep.tile([P, OUT, Q], BF16, name="bias_cand")
+                    nc.sync.dma_start(
+                        out=bias[CAND][:].rearrange("p m a -> p (m a)"),
+                        in_=Uc_b.rearrange("m a -> (m a)").partition_broadcast(P),
+                    )
+                    for g in (F_GATE, I_GATE, O_GATE):
+                        bias[g] = keep.tile([P, OUT], BF16, name="bias_gate%d" % g)
+                        nc.sync.dma_start(out=bias[g][:], in_=gate_bias[g].partition_broadcast(P))
+                    nc.sync.dma_start(out=c_raw[:], in_=c.rearrange("(p t) m a -> p t (m a)", t=BT))
+                w = weights[u // PARTS][(u % PARTS) // (PARTS // 2)]
+                first = UNIT * (u % (PARTS // 2))
+                raw = raw_pool.tile([P, UNIT, ROWS, FEAT], BF16, name="raw_unit", tag="raw_unit")
+                nc.sync.dma_start(
+                    out=raw[:].rearrange("p c j n -> p c (j n)"),
+                    in_=w[first : first + UNIT].rearrange("c (p j) n -> p c (j n)", j=ROWS),
+                )
+                raw_units.append(raw)
+
+            def prepare_input(name):
+                planes = prep.tile([P, BT, Q, FEAT], BF16, name="planes_" + name)
+                by_plane = act_raw[name][:].rearrange("p t (n a) -> p t a n", a=Q)
+                nc.vector.tensor_copy(out=planes[:, 0], in_=by_plane[:, 0])
+                nc.scalar.copy(out=planes[:, 1, Q // 2 :], in_=by_plane[:, 1, Q // 2 :])
+                nc.vector.tensor_copy(out=planes[:, 1, : Q // 2], in_=by_plane[:, 1, : Q // 2])
+                plane_words = planes[:].bitcast(F32)
+                grouped = prep.tile([P, VERSIONS, BT, P, PACK], BF16, name="grouped_" + name, align_bytes=64)
+                grouped_words = grouped[:].bitcast(F32)
+                for bt in range(BT):
+                    for a0 in range(0, Q, 2):
+                        flipped = flip_pool.tile([P, BANK], F32, name="flipped", tag="flip")
+                        for a in range(2):
+                            for u in range(HALVES):
+                                block = HALVES * a + u
+                                nc.tensor.transpose(
+                                    flipped[:, block * P : (block + 1) * P],
+                                    plane_words[:, bt, a0 + a, u * P : (u + 1) * P],
+                                    ident[:],
+                                )
+                        copy = nc.scalar.copy if a0 == 0 else nc.vector.tensor_copy
+                        copy(
+                            out=grouped_words[:, a0 : a0 + 2, bt],
+                            in_=flipped[:].rearrange("p (a u b) -> p a b u", a=2, u=HALVES),
+                        )
+                nc.vector.tensor_scalar_mul(
+                    out=grouped[:, Q:VERSIONS].rearrange("p s t b k -> p (s t b k)"),
+                    in0=grouped[:, 1:Q].rearrange("p s t b k -> p (s t b k)"),
+                    scalar1=-1.0,
+                )
+                codes = keep.tile([P, VERSIONS, BT, P], U32, name="codes_" + name, align_bytes=64)
+                scales = keep.tile([P, VERSIONS, BT, P], U8, name="scales_" + name, align_bytes=64)
+                for first, count in ((0, 4), (4, 2), (6, 1)):
+                    nc.vector.quantize_mx(
+                        out=codes[:, first : first + count].rearrange("p s t b -> p (s t b)").bitcast(FP8X4),
+                        scales=scales[:, first : first + count].rearrange("p s t b -> p (s t b)"),
+                        in_=grouped[:, first : first + count].rearrange("p s t b k -> p (s t b k)"),
+                    )
+                act_codes[name] = codes
+                act_scales[name] = scales
+
+            cand_acc = [new_acc() for d in range(Q)]
+
+            def candidate_quad(n):
+                for d in range(Q):
+                    multiply(cand_acc[d][:], d, 0, CAND * PARTS + n // UNIT, n % UNIT, whole)
+
+            first_round = [UNIT * u for u in range(PARTS)] + [UNIT * PARTS + g for g in range(n_units - PARTS)]
+
+            def prepare_ahead(n):
+                for u in range(n_units):
+                    if first_round[u] == n + LEAD:
+                        transpose_unit(u)
+                    if first_round[u] == n + 1:
+                        quantise_unit(u)
+
+            prepare_input("x")
+            for n in range(-LEAD, 0):
+                prepare_ahead(n)
+            for n in range(UNIT):
+                prepare_ahead(n)
+                candidate_quad(n)
+            prepare_input("h")
+
+        cell_pool = stack.enter_context(tc.tile_pool(name="cell", bufs=BT))
+
+        def over_components(gate, cols):
+            m0, width = cols
+            return gate[:, m0 : m0 + width].unsqueeze(2).to_broadcast([P, width, Q])
+
+        open_gate = {}
+
+        def sigmoid_gate(stage):
+            gates[stage] = []
+            for bt in range(BT):
+                gate = cell_pool.tile([P, OUT], F32, name="gate%d" % stage, tag="gate%d" % stage)
+                nc.vector.tensor_tensor(out=gate[:], in0=open_gate[stage][bt][:], in1=bias[stage][:], op=ALU.add)
+                nc.scalar.activation(out=gate[:], in_=gate[:], func=ACT.Sigmoid)
+                gates[stage].append(gate)
+
+        def keep_old(bt, f_gate):
+            cell = cell_pool.tile([P, OUT, Q], F32, name="cell", tag="cell")
+            nc.vector.tensor_tensor(
+                out=cell[:],
+                in0=over_components(f_gate, whole),
+                in1=c_raw[:, bt].rearrange("p (m a) -> p m a", a=Q),
+                op=ALU.mult,
+            )
+            return cell
+
+        cand = [cell_pool.tile([P, Q, OUT], F32, name="cand", tag="cand") for bt in range(BT)]
+        fresh = [cell_pool.tile([P, OUT, Q], F32, name="fresh", tag="fresh") for bt in range(BT)]
+        squashed = [cell_pool.tile([P, OUT, Q], F32, name="squashed", tag="squashed") for bt in range(BT)]
+        cell = []
+        gates = {}
+
+        def take_new(bt, cols):
+            m0, width = cols
+            nc.vector.tensor_tensor(
+                out=fresh[bt][:, m0 : m0 + width],
+                in0=over_components(gates[I_GATE][bt], cols),
+                in1=cand[bt][:, :, m0 : m0 + width].rearrange("p a m -> p m a"),
+                op=ALU.mult,
+            )
+
+        def new_cell(bt, cols):
+            m0, width = cols
+            part_of_cell = cell[bt][:, m0 : m0 + width]
+            nc.vector.tensor_tensor(out=part_of_cell, in0=part_of_cell, in1=fresh[bt][:, m0 : m0 + width], op=ALU.add)
+            nc.sync.dma_start(
+                out=c_rows[:, bt, m0 * Q : (m0 + width) * Q], in_=part_of_cell.rearrange("p m a -> p (m a)")
+            )
+            nc.scalar.activation(out=squashed[bt][:, m0 : m0 + width], in_=part_of_cell, func=ACT.Tanh)
+
+        def new_hidden(bt, cols):
+            m0, width = cols
+            part_of_hidden = squashed[bt][:, m0 : m0 + width]
+            nc.vector.tensor_tensor(
+                out=part_of_hidden, in0=over_components(gates[O_GATE][bt], cols), in1=part_of_hidden, op=ALU.mult
+            )
+            nc.sync.dma_start(
+                out=h_rows[:, bt, m0 * Q : (m0 + width) * Q], in_=part_of_hidden.rearrange("p m a -> p (m a)")
+            )
+
+        for n in range(UNIT, UNIT * PARTS):
+            prepare_ahead(n)
+            candidate_quad(n)
+
+        def candidate_plane(d):
+            nc.vector.tensor_tensor(out=cand[0][:, d, :], in0=cand_acc[d][:], in1=bias[CAND][:, :, d], op=ALU.add)
+            nc.scalar.activation(out=cand[0][:, d, :], in_=cand[0][:, d, :], func=ACT.Tanh)
+
+        for stage in (F_GATE, I_GATE, O_GATE):
+            accs = [new_acc() for bt in range(BT)]
+            for part in range(PARTS):
+                prepare_ahead(first_round[stage * PARTS + part])
+                for comp in range(UNIT):
+                    for bt in range(BT):
+                        multiply(accs[bt][:], 0, bt, stage * PARTS + part, comp, whole)
+                if stage == F_GATE:
+                    candidate_plane(part)
+                if stage == I_GATE and 1 <= part <= BT:
+                    cell.append(keep_old(part - 1, gates[F_GATE][part - 1]))
+                if stage == O_GATE and 1 <= part <= 2:
+                    take_new(0, halves[part - 1])
+                if stage == O_GATE and part == 3:
+                    new_cell(0, whole)
+                if part == 0 and stage > F_GATE:
+                    sigmoid_gate(stage - 1)
+            open_gate[stage] = accs
+        sigmoid_gate(O_GATE)
+
+        pieces = [(m0, CHUNK) for m0 in range(0, OUT, CHUNK)]
+        for n in range(len(pieces) + 2):
+            if n < len(pieces):
+                m0 = pieces[n][0]
+                acc = new_acc()
+                for d in range(Q):
+                    for part in range(PARTS):
+                        for comp in range(UNIT):
+                            multiply(acc[:, d * CHUNK : (d + 1) * CHUNK], d, 1, CAND * PARTS + part, comp, pieces[n])
+                nc.vector.tensor_tensor(
+                    out=cand[1][:, :, m0 : m0 + CHUNK],
+                    in0=acc[:].rearrange("p (a m) -> p a m", a=Q),
+                    in1=bias[CAND][:, m0 : m0 + CHUNK, :].rearrange("p m a -> p a m"),
+                    op=ALU.add,
+                )
+                nc.scalar.activation(
+                    out=cand[1][:, :, m0 : m0 + CHUNK], in_=cand[1][:, :, m0 : m0 + CHUNK], func=ACT.Tanh
+                )
+            if n < len(halves):
+                new_hidden(0, halves[n])
+            if 1 <= n <= len(pieces):
+                take_new(1, pieces[n - 1])
+                new_cell(1, pieces[n - 1])
+            if n >= 2:
+                new_hidden(1, pieces[n - 2])

@@ -57,18 +57,41 @@ def tile_quaternionlstmcell_pa_kernel(
         keep = stack.enter_context(tc.tile_pool(name="keep", bufs=1))
         raw_pool = stack.enter_context(tc.tile_pool(name="raw", bufs=5))
         grouped_pool = stack.enter_context(tc.tile_pool(name="grouped", bufs=3))
-        gate_q_pool = stack.enter_context(tc.tile_pool(name="gate_q", bufs=7))
+        gate_q_pool = stack.enter_context(tc.tile_pool(name="gate_q", bufs=4))
         cand_q_pool = stack.enter_context(tc.tile_pool(name="cand_q", bufs=PARTS))
         flip_pool = stack.enter_context(tc.psum_pool(name="flip", bufs=4))
         acc_pool = stack.enter_context(tc.psum_pool(name="acc", bufs=4))
 
+        bias_in = keep.tile([P, len(weights), OUT], BF16)
+        nc.vector.memset(bias_in[:], 0.0)
+        nc.sync.dma_start(out=bias_in[0:Q, CAND, :], in_=Uc_b.rearrange("(r m) a -> r (m a)", r=Q))
+        for g in (F_GATE, I_GATE, O_GATE):
+            nc.sync.dma_start(out=bias_in[0:1, g, :], in_=gate_bias[g].rearrange("(o m) -> o m", o=1))
+        pick = keep.tile([P, P], BF16)
+        make_identity(nc, pick[:])
         ident = keep.tile([P, P], F32)
         make_identity(nc, ident[:])
         warm = keep.tile([P, 1], F32)
         nc.vector.memset(warm[:], 0.0)
         nc.scalar.activation(out=warm[:], in_=warm[:], func=ACT.Sigmoid)
 
-        bias = {}
+        bias = {CAND: keep.tile([P, Q, OUT], BF16, name="bias_cand")}
+        for r in range(Q):
+            spread = flip_pool.tile([P, BANK], F32, name="spread", tag="flip")
+            nc.tensor.matmul(
+                out=spread[:], lhsT=pick[:, r : r + 1].to_broadcast([P, P]), rhs=bias_in[:, CAND, :], start=True, stop=True
+            )
+            copy = nc.vector.tensor_copy if r % 2 == 0 else nc.scalar.copy
+            copy(out=bias[CAND][:, :, r * P : (r + 1) * P], in_=spread[:].rearrange("p (m a) -> p a m", a=Q))
+        for g in (F_GATE, I_GATE, O_GATE):
+            bias[g] = keep.tile([P, OUT], BF16, name="bias_gate%d" % g)
+            spread = flip_pool.tile([P, BANK], F32, name="spread", tag="flip")
+            nc.tensor.matmul(
+                out=spread[:], lhsT=pick[:, 0:1].to_broadcast([P, P]), rhs=bias_in[:, g, :], start=True, stop=True
+            )
+            copy = nc.vector.tensor_copy if g % 2 == 0 else nc.scalar.copy
+            copy(out=bias[g][:], in_=spread[:])
+
         c_raw = keep.tile([P, BT, OUT * Q], BF16)
         act_raw = {}
         act_codes = {}
@@ -143,14 +166,6 @@ def tile_quaternionlstmcell_pa_kernel(
                 if u == PARTS // 2:
                     load_input("h", h)
                 if u == PARTS + PARTS // 2:
-                    bias[CAND] = keep.tile([P, OUT, Q], BF16, name="bias_cand")
-                    nc.sync.dma_start(
-                        out=bias[CAND][:].rearrange("p m a -> p (m a)"),
-                        in_=Uc_b.rearrange("m a -> (m a)").partition_broadcast(P),
-                    )
-                    for g in (F_GATE, I_GATE, O_GATE):
-                        bias[g] = keep.tile([P, OUT], BF16, name="bias_gate%d" % g)
-                        nc.sync.dma_start(out=bias[g][:], in_=gate_bias[g].partition_broadcast(P))
                     nc.sync.dma_start(out=c_raw[:], in_=c.rearrange("(p t) m a -> p t (m a)", t=BT))
                 w = weights[u // PARTS][(u % PARTS) // (PARTS // 2)]
                 first = UNIT * (u % (PARTS // 2))
@@ -290,7 +305,7 @@ def tile_quaternionlstmcell_pa_kernel(
             candidate_quad(n)
 
         def candidate_plane(d):
-            nc.vector.tensor_tensor(out=cand[0][:, d, :], in0=cand_acc[d][:], in1=bias[CAND][:, :, d], op=ALU.add)
+            nc.vector.tensor_tensor(out=cand[0][:, d, :], in0=cand_acc[d][:], in1=bias[CAND][:, d, :], op=ALU.add)
             nc.scalar.activation(out=cand[0][:, d, :], in_=cand[0][:, d, :], func=ACT.Tanh)
 
         for stage in (F_GATE, I_GATE, O_GATE):
@@ -325,7 +340,7 @@ def tile_quaternionlstmcell_pa_kernel(
                 nc.vector.tensor_tensor(
                     out=cand[1][:, :, m0 : m0 + CHUNK],
                     in0=acc[:].rearrange("p (a m) -> p a m", a=Q),
-                    in1=bias[CAND][:, m0 : m0 + CHUNK, :].rearrange("p m a -> p a m"),
+                    in1=bias[CAND][:, :, m0 : m0 + CHUNK],
                     op=ALU.add,
                 )
                 nc.scalar.activation(

@@ -62,36 +62,13 @@ def tile_quaternionlstmcell_pa_kernel(
         flip_pool = stack.enter_context(tc.psum_pool(name="flip", bufs=4))
         acc_pool = stack.enter_context(tc.psum_pool(name="acc", bufs=4))
 
-        bias_in = keep.tile([P, len(weights), OUT], BF16)
-        nc.vector.memset(bias_in[:], 0.0)
-        nc.sync.dma_start(out=bias_in[0:Q, CAND, :], in_=Uc_b.rearrange("(r m) a -> r (m a)", r=Q))
-        for g in (F_GATE, I_GATE, O_GATE):
-            nc.sync.dma_start(out=bias_in[0:1, g, :], in_=gate_bias[g].rearrange("(o m) -> o m", o=1))
-        pick = keep.tile([P, P], BF16)
-        make_identity(nc, pick[:])
         ident = keep.tile([P, P], F32)
         make_identity(nc, ident[:])
         warm = keep.tile([P, 1], F32)
         nc.vector.memset(warm[:], 0.0)
         nc.scalar.activation(out=warm[:], in_=warm[:], func=ACT.Sigmoid)
 
-        bias = {CAND: keep.tile([P, Q, OUT], BF16, name="bias_cand")}
-        for r in range(Q):
-            spread = flip_pool.tile([P, BANK], F32, name="spread", tag="flip")
-            nc.tensor.matmul(
-                out=spread[:], lhsT=pick[:, r : r + 1].to_broadcast([P, P]), rhs=bias_in[:, CAND, :], start=True, stop=True
-            )
-            copy = nc.vector.tensor_copy if r % 2 == 0 else nc.scalar.copy
-            copy(out=bias[CAND][:, :, r * P : (r + 1) * P], in_=spread[:].rearrange("p (m a) -> p a m", a=Q))
-        for g in (F_GATE, I_GATE, O_GATE):
-            bias[g] = keep.tile([P, OUT], BF16, name="bias_gate%d" % g)
-            spread = flip_pool.tile([P, BANK], F32, name="spread", tag="flip")
-            nc.tensor.matmul(
-                out=spread[:], lhsT=pick[:, 0:1].to_broadcast([P, P]), rhs=bias_in[:, g, :], start=True, stop=True
-            )
-            copy = nc.vector.tensor_copy if g % 2 == 0 else nc.scalar.copy
-            copy(out=bias[g][:], in_=spread[:])
-
+        bias = {}
         c_raw = keep.tile([P, BT, OUT * Q], BF16)
         act_raw = {}
         act_codes = {}
@@ -166,6 +143,14 @@ def tile_quaternionlstmcell_pa_kernel(
                 if u == PARTS // 2:
                     load_input("h", h)
                 if u == PARTS + PARTS // 2:
+                    bias[CAND] = keep.tile([P, OUT, Q], BF16, name="bias_cand")
+                    nc.sync.dma_start(
+                        out=bias[CAND][:].rearrange("p m a -> p (m a)"),
+                        in_=Uc_b.rearrange("m a -> (m a)").partition_broadcast(P),
+                    )
+                    for g in (F_GATE, I_GATE, O_GATE):
+                        bias[g] = keep.tile([P, OUT], BF16, name="bias_gate%d" % g)
+                        nc.sync.dma_start(out=bias[g][:], in_=gate_bias[g].partition_broadcast(P))
                     nc.sync.dma_start(out=c_raw[:], in_=c.rearrange("(p t) m a -> p t (m a)", t=BT))
                 w = weights[u // PARTS][(u % PARTS) // (PARTS // 2)]
                 first = UNIT * (u % (PARTS // 2))
@@ -201,14 +186,15 @@ def tile_quaternionlstmcell_pa_kernel(
                             out=grouped_words[:, a0 : a0 + 2, bt],
                             in_=flipped[:].rearrange("p (a u b) -> p a b u", a=2, u=HALVES),
                         )
-                nc.vector.tensor_scalar_mul(
-                    out=grouped[:, Q:VERSIONS].rearrange("p s t b k -> p (s t b k)"),
-                    in0=grouped[:, 1:Q].rearrange("p s t b k -> p (s t b k)"),
-                    scalar1=-1.0,
-                )
                 codes = keep.tile([P, VERSIONS, BT, P], U32, name="codes_" + name, align_bytes=64)
                 scales = keep.tile([P, VERSIONS, BT, P], U8, name="scales_" + name, align_bytes=64)
                 for first, count in ((0, 4), (4, 2), (6, 1)):
+                    if first == Q:
+                        nc.vector.tensor_scalar_mul(
+                            out=grouped[:, Q:VERSIONS].rearrange("p s t b k -> p (s t b k)"),
+                            in0=grouped[:, 1:Q].rearrange("p s t b k -> p (s t b k)"),
+                            scalar1=-1.0,
+                        )
                     nc.vector.quantize_mx(
                         out=codes[:, first : first + count].rearrange("p s t b -> p (s t b)").bitcast(FP8X4),
                         scales=scales[:, first : first + count].rearrange("p s t b -> p (s t b)"),
@@ -266,18 +252,19 @@ def tile_quaternionlstmcell_pa_kernel(
             )
             return cell
 
-        cand = [cell_pool.tile([P, Q, OUT], F32, name="cand", tag="cand") for bt in range(BT)]
+        cand = cell_pool.tile([P, Q, OUT], F32, name="cand", tag="cand", bufs=1)
+        cand_pieces = []
         fresh = [cell_pool.tile([P, OUT, Q], F32, name="fresh", tag="fresh") for bt in range(BT)]
         squashed = [cell_pool.tile([P, OUT, Q], F32, name="squashed", tag="squashed") for bt in range(BT)]
         cell = []
         gates = {}
 
-        def take_new(bt, cols):
+        def take_new(bt, cols, planes):
             m0, width = cols
             nc.vector.tensor_tensor(
                 out=fresh[bt][:, m0 : m0 + width],
                 in0=over_components(gates[I_GATE][bt], cols),
-                in1=cand[bt][:, :, m0 : m0 + width].rearrange("p a m -> p m a"),
+                in1=planes.rearrange("p a m -> p m a"),
                 op=ALU.mult,
             )
 
@@ -300,27 +287,52 @@ def tile_quaternionlstmcell_pa_kernel(
                 out=h_rows[:, bt, m0 * Q : (m0 + width) * Q], in_=part_of_hidden.rearrange("p m a -> p (m a)")
             )
 
+        pieces = [(m0, CHUNK) for m0 in range(0, OUT, CHUNK)]
+
+        def piece_passes(n):
+            m0 = pieces[n][0]
+            acc = new_acc()
+            for d in range(Q):
+                for part in range(PARTS):
+                    for comp in range(UNIT):
+                        multiply(acc[:, d * CHUNK : (d + 1) * CHUNK], d, 1, CAND * PARTS + part, comp, pieces[n])
+            piece = cell_pool.tile([P, Q, CHUNK], F32, name="cand_piece", tag="cand_piece")
+            nc.vector.tensor_tensor(
+                out=piece[:],
+                in0=acc[:].rearrange("p (a m) -> p a m", a=Q),
+                in1=bias[CAND][:, m0 : m0 + CHUNK, :].rearrange("p m a -> p a m"),
+                op=ALU.add,
+            )
+            nc.scalar.activation(out=piece[:], in_=piece[:], func=ACT.Tanh)
+            cand_pieces.append(piece)
+
         for n in range(UNIT, UNIT * PARTS):
             prepare_ahead(n)
             candidate_quad(n)
 
         def candidate_plane(d):
-            nc.vector.tensor_tensor(out=cand[0][:, d, :], in0=cand_acc[d][:], in1=bias[CAND][:, d, :], op=ALU.add)
-            nc.scalar.activation(out=cand[0][:, d, :], in_=cand[0][:, d, :], func=ACT.Tanh)
+            nc.vector.tensor_tensor(out=cand[:, d, :], in0=cand_acc[d][:], in1=bias[CAND][:, :, d], op=ALU.add)
+            nc.scalar.activation(out=cand[:, d, :], in_=cand[:, d, :], func=ACT.Tanh)
+
+        for d in range(BT):
+            candidate_plane(d)
 
         for stage in (F_GATE, I_GATE, O_GATE):
             accs = [new_acc() for bt in range(BT)]
             for part in range(PARTS):
+                if stage == O_GATE and part == PARTS - 1:
+                    piece_passes(0)
                 prepare_ahead(first_round[stage * PARTS + part])
                 for comp in range(UNIT):
                     for bt in range(BT):
                         multiply(accs[bt][:], 0, bt, stage * PARTS + part, comp, whole)
-                if stage == F_GATE:
-                    candidate_plane(part)
+                if stage == F_GATE and part < Q - BT:
+                    candidate_plane(BT + part)
                 if stage == I_GATE and 1 <= part <= BT:
                     cell.append(keep_old(part - 1, gates[F_GATE][part - 1]))
                 if stage == O_GATE and 1 <= part <= 2:
-                    take_new(0, halves[part - 1])
+                    m0, width = halves[part - 1]
+                    take_new(0, halves[part - 1], cand[:, :, m0 : m0 + width])
                 if stage == O_GATE and part == 3:
                     new_cell(0, whole)
                 if part == 0 and stage > F_GATE:
@@ -328,28 +340,13 @@ def tile_quaternionlstmcell_pa_kernel(
             open_gate[stage] = accs
         sigmoid_gate(O_GATE)
 
-        pieces = [(m0, CHUNK) for m0 in range(0, OUT, CHUNK)]
         for n in range(len(pieces) + 2):
-            if n < len(pieces):
-                m0 = pieces[n][0]
-                acc = new_acc()
-                for d in range(Q):
-                    for part in range(PARTS):
-                        for comp in range(UNIT):
-                            multiply(acc[:, d * CHUNK : (d + 1) * CHUNK], d, 1, CAND * PARTS + part, comp, pieces[n])
-                nc.vector.tensor_tensor(
-                    out=cand[1][:, :, m0 : m0 + CHUNK],
-                    in0=acc[:].rearrange("p (a m) -> p a m", a=Q),
-                    in1=bias[CAND][:, :, m0 : m0 + CHUNK],
-                    op=ALU.add,
-                )
-                nc.scalar.activation(
-                    out=cand[1][:, :, m0 : m0 + CHUNK], in_=cand[1][:, :, m0 : m0 + CHUNK], func=ACT.Tanh
-                )
-            if n < len(halves):
-                new_hidden(0, halves[n])
+            if 1 <= n < len(pieces):
+                piece_passes(n)
             if 1 <= n <= len(pieces):
-                take_new(1, pieces[n - 1])
+                take_new(1, pieces[n - 1], cand_pieces[n - 1][:])
                 new_cell(1, pieces[n - 1])
             if n >= 2:
                 new_hidden(1, pieces[n - 2])
+            if 1 <= n <= len(halves):
+                new_hidden(0, halves[n - 1])

@@ -71,6 +71,7 @@ def tile_quaternionlstmcell_pa_kernel(
         bias = {}
         c_raw = keep.tile([P, BT, OUT * Q], BF16)
         act_raw = {}
+        act_grouped = {}
         act_codes = {}
         act_scales = {}
         raw_units = []
@@ -136,7 +137,9 @@ def tile_quaternionlstmcell_pa_kernel(
         with tc.tile_pool(name="prep", bufs=1) as prep:
             def load_input(name, v):
                 act_raw[name] = prep.tile([P, BT, FEAT * Q], BF16, name="raw_" + name)
-                nc.sync.dma_start(out=act_raw[name][:], in_=v.rearrange("(p t) n a -> p t (n a)", t=BT))
+                rows = v.rearrange("(p t) n a -> p t (n a)", t=BT)
+                for bt in range(BT):
+                    nc.sync.dma_start(out=act_raw[name][:, bt], in_=rows[:, bt])
 
             load_input("x", x)
             for u in range(n_units):
@@ -161,13 +164,18 @@ def tile_quaternionlstmcell_pa_kernel(
                 )
                 raw_units.append(raw)
 
-            def prepare_input(name):
+            act_planes = {}
+
+            def split_input(name):
                 planes = prep.tile([P, BT, Q, FEAT], BF16, name="planes_" + name)
+                act_planes[name] = planes
                 by_plane = act_raw[name][:].rearrange("p t (n a) -> p t a n", a=Q)
                 nc.vector.tensor_copy(out=planes[:, 0], in_=by_plane[:, 0])
                 nc.scalar.copy(out=planes[:, 1, Q // 2 :], in_=by_plane[:, 1, Q // 2 :])
                 nc.vector.tensor_copy(out=planes[:, 1, : Q // 2], in_=by_plane[:, 1, : Q // 2])
-                plane_words = planes[:].bitcast(F32)
+
+            def flip_input(name):
+                plane_words = act_planes[name][:].bitcast(F32)
                 grouped = prep.tile([P, VERSIONS, BT, P, PACK], BF16, name="grouped_" + name, align_bytes=64)
                 grouped_words = grouped[:].bitcast(F32)
                 for bt in range(BT):
@@ -188,20 +196,26 @@ def tile_quaternionlstmcell_pa_kernel(
                         )
                 codes = keep.tile([P, VERSIONS, BT, P], U32, name="codes_" + name, align_bytes=64)
                 scales = keep.tile([P, VERSIONS, BT, P], U8, name="scales_" + name, align_bytes=64)
-                for first, count in ((0, 4), (4, 2), (6, 1)):
-                    if first == Q:
-                        nc.vector.tensor_scalar_mul(
-                            out=grouped[:, Q:VERSIONS].rearrange("p s t b k -> p (s t b k)"),
-                            in0=grouped[:, 1:Q].rearrange("p s t b k -> p (s t b k)"),
-                            scalar1=-1.0,
-                        )
-                    nc.vector.quantize_mx(
-                        out=codes[:, first : first + count].rearrange("p s t b -> p (s t b)").bitcast(FP8X4),
-                        scales=scales[:, first : first + count].rearrange("p s t b -> p (s t b)"),
-                        in_=grouped[:, first : first + count].rearrange("p s t b k -> p (s t b k)"),
-                    )
+                act_grouped[name] = grouped
                 act_codes[name] = codes
                 act_scales[name] = scales
+                quantise_versions(name, 0, Q)
+                nc.vector.tensor_scalar_mul(
+                    out=grouped[:, Q:VERSIONS].rearrange("p s t b k -> p (s t b k)"),
+                    in0=grouped[:, 1:Q].rearrange("p s t b k -> p (s t b k)"),
+                    scalar1=-1.0,
+                )
+
+            def quantise_versions(name, first, count):
+                nc.vector.quantize_mx(
+                    out=act_codes[name][:, first : first + count].rearrange("p s t b -> p (s t b)").bitcast(FP8X4),
+                    scales=act_scales[name][:, first : first + count].rearrange("p s t b -> p (s t b)"),
+                    in_=act_grouped[name][:, first : first + count].rearrange("p s t b k -> p (s t b k)"),
+                )
+
+            def quantise_negated(name):
+                quantise_versions(name, Q, 2)
+                quantise_versions(name, Q + 2, 1)
 
             cand_acc = [new_acc() for d in range(Q)]
 
@@ -218,13 +232,19 @@ def tile_quaternionlstmcell_pa_kernel(
                     if first_round[u] == n + 1:
                         quantise_unit(u)
 
-            prepare_input("x")
+            split_input("x")
+            flip_input("x")
             for n in range(-LEAD, 0):
                 prepare_ahead(n)
-            for n in range(UNIT):
+            quantise_negated("x")
+            for n in range(UNIT * PARTS // 2):
                 prepare_ahead(n)
+                if n == 3:
+                    flip_input("h")
                 candidate_quad(n)
-            prepare_input("h")
+                if n == 1:
+                    split_input("h")
+            quantise_negated("h")
 
         cell_pool = stack.enter_context(tc.tile_pool(name="cell", bufs=BT))
 
@@ -275,7 +295,12 @@ def tile_quaternionlstmcell_pa_kernel(
             nc.sync.dma_start(
                 out=c_rows[:, bt, m0 * Q : (m0 + width) * Q], in_=part_of_cell.rearrange("p m a -> p (m a)")
             )
-            nc.scalar.activation(out=squashed[bt][:, m0 : m0 + width], in_=part_of_cell, func=ACT.Tanh)
+
+        def squash(bt, cols):
+            m0, width = cols
+            nc.scalar.activation(
+                out=squashed[bt][:, m0 : m0 + width], in_=cell[bt][:, m0 : m0 + width], func=ACT.Tanh
+            )
 
         def new_hidden(bt, cols):
             m0, width = cols
@@ -289,13 +314,19 @@ def tile_quaternionlstmcell_pa_kernel(
 
         pieces = [(m0, CHUNK) for m0 in range(0, OUT, CHUNK)]
 
+        piece_acc = []
+
         def piece_passes(n):
-            m0 = pieces[n][0]
             acc = new_acc()
             for d in range(Q):
                 for part in range(PARTS):
                     for comp in range(UNIT):
                         multiply(acc[:, d * CHUNK : (d + 1) * CHUNK], d, 1, CAND * PARTS + part, comp, pieces[n])
+            piece_acc.append(acc)
+
+        def piece_candidate(n):
+            m0 = pieces[n][0]
+            acc = piece_acc[n]
             piece = cell_pool.tile([P, Q, CHUNK], F32, name="cand_piece", tag="cand_piece")
             nc.vector.tensor_tensor(
                 out=piece[:],
@@ -306,7 +337,7 @@ def tile_quaternionlstmcell_pa_kernel(
             nc.scalar.activation(out=piece[:], in_=piece[:], func=ACT.Tanh)
             cand_pieces.append(piece)
 
-        for n in range(UNIT, UNIT * PARTS):
+        for n in range(UNIT * PARTS // 2, UNIT * PARTS):
             prepare_ahead(n)
             candidate_quad(n)
 
@@ -330,15 +361,17 @@ def tile_quaternionlstmcell_pa_kernel(
                     candidate_plane(BT + part)
                 if stage == I_GATE and 1 <= part <= BT:
                     cell.append(keep_old(part - 1, gates[F_GATE][part - 1]))
-                if stage == O_GATE and 1 <= part <= 2:
-                    m0, width = halves[part - 1]
-                    take_new(0, halves[part - 1], cand[:, :, m0 : m0 + width])
-                if stage == O_GATE and part == 3:
+                if stage == O_GATE and part == 1:
+                    take_new(0, whole, cand[:])
+                if stage == O_GATE and part == 2:
                     new_cell(0, whole)
+                if stage == O_GATE and part == PARTS - 1:
+                    piece_candidate(0)
                 if part == 0 and stage > F_GATE:
                     sigmoid_gate(stage - 1)
             open_gate[stage] = accs
         sigmoid_gate(O_GATE)
+        squash(0, halves[0])
 
         for n in range(len(pieces) + 2):
             if 1 <= n < len(pieces):
@@ -346,7 +379,12 @@ def tile_quaternionlstmcell_pa_kernel(
             if 1 <= n <= len(pieces):
                 take_new(1, pieces[n - 1], cand_pieces[n - 1][:])
                 new_cell(1, pieces[n - 1])
+                squash(1, pieces[n - 1])
+            if 1 <= n < len(pieces):
+                piece_candidate(n)
             if n >= 2:
                 new_hidden(1, pieces[n - 2])
             if 1 <= n <= len(halves):
                 new_hidden(0, halves[n - 1])
+                if n < len(halves):
+                    squash(0, halves[n])

@@ -17,9 +17,10 @@ BATCH, FEAT, OUT, Q = 256, 512, 512, 4
 BT = BATCH // P
 WORDS = FEAT // 2
 HALVES = WORDS // P
-ROWS = OUT // P
 BANK = 512
 UNIT = 2
+SPAN = P // UNIT
+ROWS = OUT // SPAN
 PARTS = 2 * Q // UNIT
 VERSIONS = 2 * Q - 1
 CHUNK = BANK // Q
@@ -55,7 +56,7 @@ def tile_quaternionlstmcell_pa_kernel(
     with ExitStack() as stack:
         stack.enter_context(tc.manual_schedule())
         keep = stack.enter_context(tc.tile_pool(name="keep", bufs=1))
-        raw_pool = stack.enter_context(tc.tile_pool(name="raw", bufs=5))
+        raw_pool = stack.enter_context(tc.tile_pool(name="raw", bufs=8))
         grouped_pool = stack.enter_context(tc.tile_pool(name="grouped", bufs=3))
         gate_q_pool = stack.enter_context(tc.tile_pool(name="gate_q", bufs=4))
         cand_q_pool = stack.enter_context(tc.tile_pool(name="cand_q", bufs=PARTS))
@@ -82,22 +83,21 @@ def tile_quaternionlstmcell_pa_kernel(
         def transpose_unit(u):
             raw_words = raw_units[u][:].bitcast(F32)
             grouped = grouped_pool.tile([P, UNIT, OUT, PACK], BF16, name="grouped_unit", tag="grouped_unit", align_bytes=64)
-            grouped_words = grouped[:].bitcast(F32)
-            for comp in range(UNIT):
-                for j0 in range(0, ROWS, 2):
-                    flipped = flip_pool.tile([P, BANK], F32, name="flipped", tag="flip")
-                    for j in range(2):
-                        for u2 in range(HALVES):
-                            block = HALVES * j + u2
-                            nc.tensor.transpose(
-                                flipped[:, block * P : (block + 1) * P],
-                                raw_words[:, comp, j0 + j, u2 * P : (u2 + 1) * P],
-                                ident[:],
-                            )
-                    nc.scalar.copy(
-                        out=grouped_words[:, comp].rearrange("p (q g j) u -> p g q j u", g=ROWS // 2, j=2)[:, j0 // 2],
-                        in_=flipped[:].rearrange("p (j u q) -> p q j u", j=2, u=HALVES),
-                    )
+            grouped_words = grouped[:].rearrange("p c m k -> p (c m) k").bitcast(F32)
+            for g in range(ROWS // 2):
+                flipped = flip_pool.tile([P, BANK], F32, name="flipped", tag="flip")
+                for j in range(2):
+                    for u2 in range(HALVES):
+                        block = HALVES * j + u2
+                        nc.tensor.transpose(
+                            flipped[:, block * P : (block + 1) * P],
+                            raw_words[:, 2 * g + j, u2 * P : (u2 + 1) * P],
+                            ident[:],
+                        )
+                nc.scalar.copy(
+                    out=grouped_words.rearrange("p (q g j) u -> p g q j u", g=ROWS // 2, j=2)[:, g],
+                    in_=flipped[:].rearrange("p (j u q) -> p q j u", j=2, u=HALVES),
+                )
             grouped_units[u] = grouped
 
         def quantise_unit(u):
@@ -145,22 +145,24 @@ def tile_quaternionlstmcell_pa_kernel(
             for u in range(n_units):
                 if u == PARTS // 2:
                     load_input("h", h)
-                if u == PARTS + PARTS // 2:
+                if u == 5:
                     bias[CAND] = keep.tile([P, OUT, Q], BF16, name="bias_cand")
                     nc.sync.dma_start(
                         out=bias[CAND][:].rearrange("p m a -> p (m a)"),
                         in_=Uc_b.rearrange("m a -> (m a)").partition_broadcast(P),
                     )
+                if u == 9:
                     for g in (F_GATE, I_GATE, O_GATE):
                         bias[g] = keep.tile([P, OUT], BF16, name="bias_gate%d" % g)
                         nc.sync.dma_start(out=bias[g][:], in_=gate_bias[g].partition_broadcast(P))
+                if u == 11:
                     nc.sync.dma_start(out=c_raw[:], in_=c.rearrange("(p t) m a -> p t (m a)", t=BT))
                 w = weights[u // PARTS][(u % PARTS) // (PARTS // 2)]
                 first = UNIT * (u % (PARTS // 2))
-                raw = raw_pool.tile([P, UNIT, ROWS, FEAT], BF16, name="raw_unit", tag="raw_unit")
+                raw = raw_pool.tile([P, ROWS, FEAT], BF16, name="raw_unit", tag="raw_unit")
                 nc.sync.dma_start(
-                    out=raw[:].rearrange("p c j n -> p c (j n)"),
-                    in_=w[first : first + UNIT].rearrange("c (p j) n -> p c (j n)", j=ROWS),
+                    out=raw[:].rearrange("q j n -> q (j n)"),
+                    in_=w[first : first + UNIT].rearrange("c (p j) n -> (c p) (j n)", j=ROWS),
                 )
                 raw_units.append(raw)
 

@@ -18,13 +18,14 @@ BT = BATCH // P
 WORDS = FEAT // 2
 HALVES = WORDS // P
 BANK = 512
+CHUNK = BANK // Q
+PLANES = (1, 0, 2, 3)
+COLS = BANK // BT
+PARTS = OUT // COLS
 UNIT = 2
 SPAN = P // UNIT
 ROWS = OUT // SPAN
-PARTS = 2 * Q // UNIT
 VERSIONS = 2 * Q - 1
-CHUNK = BANK // Q
-LEAD = 2
 
 HAM = (
     ((0, 1.0), (1, 1.0), (2, 1.0), (3, 1.0)),
@@ -36,11 +37,16 @@ HAM = (
 FLOPS = 2 * BATCH * FEAT * OUT * 2 * (3 * Q + Q * Q)
 
 CAND, F_GATE, I_GATE, O_GATE = 0, 1, 2, 3
+GATES = (F_GATE, I_GATE, O_GATE)
+ORDER = ((CAND, 0), (F_GATE, 0), (I_GATE, 0), (O_GATE, 0))
+V_BANKS = {}
 
 
 def input_version(d, w_comp):
     a = [a for a in range(Q) if HAM[a][d][0] == w_comp][0]
-    return a if HAM[a][d][1] > 0 else Q - 1 + a
+    if a == 0:
+        return Q - 1
+    return a - 1 if HAM[a][d][1] > 0 else Q - 1 + a
 
 
 def tile_quaternionlstmcell_pa_kernel(
@@ -49,17 +55,22 @@ def tile_quaternionlstmcell_pa_kernel(
     nc = tc.nc
     weights = {CAND: (Wc_w, Uc_w), F_GATE: (Wf_w, Uf_w), I_GATE: (Wi_w, Ui_w), O_GATE: (Wo_w, Uo_w)}
     gate_bias = {F_GATE: Uf_br, I_GATE: Ui_br, O_GATE: Uo_br}
-    n_units = len(weights) * PARTS
+    units = []
+    for stage, part in ORDER:
+        units += [(stage, side, c0, UNIT, 0, OUT) for side in range(2) for c0 in range(0, Q, UNIT)]
+    first_unit = {}
+    for u in range(len(units)):
+        first_unit.setdefault((units[u][0], units[u][4] // COLS), u)
     h_rows = out_0.rearrange("(p t) m a -> p t (m a)", t=BT)
     c_rows = out_1.rearrange("(p t) m a -> p t (m a)", t=BT)
 
     with ExitStack() as stack:
         stack.enter_context(tc.manual_schedule())
         keep = stack.enter_context(tc.tile_pool(name="keep", bufs=1))
-        raw_pool = stack.enter_context(tc.tile_pool(name="raw", bufs=8))
+        raw_pool = stack.enter_context(tc.tile_pool(name="raw", bufs=7))
         grouped_pool = stack.enter_context(tc.tile_pool(name="grouped", bufs=3))
-        gate_q_pool = stack.enter_context(tc.tile_pool(name="gate_q", bufs=4))
-        cand_q_pool = stack.enter_context(tc.tile_pool(name="cand_q", bufs=PARTS))
+        cand_code_pool = stack.enter_context(tc.tile_pool(name="cand_codes", bufs=4))
+        code_pool = stack.enter_context(tc.tile_pool(name="codes", bufs=4))
         flip_pool = stack.enter_context(tc.psum_pool(name="flip", bufs=4))
         acc_pool = stack.enter_context(tc.psum_pool(name="acc", bufs=4))
 
@@ -72,6 +83,7 @@ def tile_quaternionlstmcell_pa_kernel(
         bias = {}
         c_raw = keep.tile([P, BT, OUT * Q], BF16)
         act_raw = {}
+        act_planes = {}
         act_grouped = {}
         act_codes = {}
         act_scales = {}
@@ -94,14 +106,15 @@ def tile_quaternionlstmcell_pa_kernel(
                             raw_words[:, 2 * g + j, u2 * P : (u2 + 1) * P],
                             ident[:],
                         )
-                nc.scalar.copy(
+                copy = nc.vector.tensor_copy if g in V_BANKS.get(u, ()) else nc.scalar.copy
+                copy(
                     out=grouped_words.rearrange("p (q g j) u -> p g q j u", g=ROWS // 2, j=2)[:, g],
                     in_=flipped[:].rearrange("p (j u q) -> p q j u", j=2, u=HALVES),
                 )
             grouped_units[u] = grouped
 
         def quantise_unit(u):
-            pool = cand_q_pool if u // PARTS == CAND else gate_q_pool
+            pool = cand_code_pool if units[u][0] == CAND else code_pool
             codes = pool.tile([P, UNIT, OUT], U32, name="unit_codes", tag="unit_codes", align_bytes=64)
             scales = pool.tile([P, UNIT, OUT], U8, name="unit_scales", tag="unit_scales", align_bytes=64)
             nc.vector.quantize_mx(
@@ -112,27 +125,54 @@ def tile_quaternionlstmcell_pa_kernel(
             unit_codes[u] = codes
             unit_scales[u] = scales
 
-        def multiply(acc, d, bt, u, comp, cols):
-            part = u % PARTS
-            name = "x" if part < PARTS // 2 else "h"
-            version = input_version(d, UNIT * (part % (PARTS // 2)) + comp)
-            m0, width = cols
+        def multiply(acc, d, bt, u, comp, start, stop, cols=slice(0, OUT)):
+            side, c0 = units[u][1:3]
+            name = ("x", "h")[side]
+            version = input_version(d, comp)
             nc.tensor.matmul_mx(
                 out=acc,
                 lhsT=act_codes[name][:, version, bt, :].bitcast(FP8X4),
                 lhsT_scale=act_scales[name][:, version, bt, :],
-                rhs=unit_codes[u][:, comp, m0 : m0 + width].bitcast(FP8X4),
-                rhs_scale=unit_scales[u][:, comp, m0 : m0 + width],
-                start=(part == 0 and comp == 0),
-                stop=(part == PARTS - 1 and comp == UNIT - 1),
+                rhs=unit_codes[u][:, comp - c0, cols].bitcast(FP8X4),
+                rhs_scale=unit_scales[u][:, comp - c0, cols],
+                start=start,
+                stop=stop,
             )
 
         def new_acc():
             acc = acc_pool.tile([P, BANK], F32, name="acc", tag="acc")
             return acc
 
-        whole = (0, OUT)
-        halves = ((0, OUT // 2), (OUT // 2, OUT // 2))
+        def group(stage, acc, half, d, bt, part):
+            u = first_unit[stage, 0]
+            for side in range(2):
+                for comp in range(Q):
+                    first, last = side == 0 and comp == 0, side == 1 and comp == Q - 1
+                    of = u + (Q * side + comp) // UNIT
+                    multiply(acc[:, COLS * half : COLS * (half + 1)], d, bt, of, comp, first, last, columns(part))
+
+        def columns(part):
+            return slice(COLS * part, COLS * (part + 1))
+
+        cand_acc = []
+
+        def first_tile(comp, side):
+            if not cand_acc:
+                cand_acc.extend([new_acc() for d in range(Q)])
+            for d in range(Q):
+                first, last = side == 0 and comp == 0, side == 1 and comp == Q - 1
+                multiply(cand_acc[d][:], d, 0, first_unit[CAND, 0] + (Q * side + comp) // UNIT, comp, first, last)
+
+        gate_accs = {}
+
+        def gate_unit(u):
+            stage, side, c0 = units[u][:3]
+            if stage not in gate_accs:
+                gate_accs[stage] = [new_acc() for bt in range(BT)]
+            for comp in (c0, c0 + 1):
+                for bt in range(BT):
+                    first, last = side == 0 and comp == 0, side == 1 and comp == Q - 1
+                    multiply(gate_accs[stage][bt][:], 0, bt, u, comp, first, last)
 
         with tc.tile_pool(name="prep", bufs=1) as prep:
             def load_input(name, v):
@@ -141,72 +181,64 @@ def tile_quaternionlstmcell_pa_kernel(
                 for bt in range(BT):
                     nc.sync.dma_start(out=act_raw[name][:, bt], in_=rows[:, bt])
 
-            load_input("x", x)
-            for u in range(n_units):
-                if u == PARTS // 2:
+            X_AT, H_AT, BF_AT, B2_AT, C_AT, B_AT = 0, 2, 9, 5, 11, 9
+            for u in range(len(units)):
+                if u == X_AT:
+                    load_input("x", x)
+                stage, side, c0, comps, m0, cols = units[u]
+                if u == H_AT:
                     load_input("h", h)
-                if u == 5:
+                for g in ((F_GATE,) if u == BF_AT else ()) + ((I_GATE, O_GATE) if u == B_AT else ()):
+                    bias[g] = keep.tile([P, OUT], BF16, name="bias_gate%d" % g)
+                    nc.sync.dma_start(out=bias[g][:], in_=gate_bias[g].partition_broadcast(P))
+                if u == B2_AT:
                     bias[CAND] = keep.tile([P, OUT, Q], BF16, name="bias_cand")
                     nc.sync.dma_start(
                         out=bias[CAND][:].rearrange("p m a -> p (m a)"),
                         in_=Uc_b.rearrange("m a -> (m a)").partition_broadcast(P),
                     )
-                if u == 9:
-                    for g in (F_GATE, I_GATE, O_GATE):
-                        bias[g] = keep.tile([P, OUT], BF16, name="bias_gate%d" % g)
-                        nc.sync.dma_start(out=bias[g][:], in_=gate_bias[g].partition_broadcast(P))
-                if u == 11:
+                if u == C_AT:
                     nc.sync.dma_start(out=c_raw[:], in_=c.rearrange("(p t) m a -> p t (m a)", t=BT))
-                w = weights[u // PARTS][(u % PARTS) // (PARTS // 2)]
-                first = UNIT * (u % (PARTS // 2))
+                w = weights[stage][side][c0 : c0 + UNIT]
                 raw = raw_pool.tile([P, ROWS, FEAT], BF16, name="raw_unit", tag="raw_unit")
                 nc.sync.dma_start(
-                    out=raw[:].rearrange("q j n -> q (j n)"),
-                    in_=w[first : first + UNIT].rearrange("c (p j) n -> (c p) (j n)", j=ROWS),
+                    out=raw[:].rearrange("q j n -> q (j n)"), in_=w.rearrange("c (p j) n -> (c p) (j n)", j=ROWS)
                 )
                 raw_units.append(raw)
 
-            act_planes = {}
+            def split_input(name, bt, v_planes):
+                if name not in act_planes:
+                    act_planes[name] = prep.tile([P, BT, Q, FEAT], BF16, name="planes_" + name)
+                planes = act_planes[name][:, bt]
+                by_plane = act_raw[name][:, bt].rearrange("p (n a) -> p a n", a=Q)
+                if v_planes > 0:
+                    nc.vector.tensor_copy(out=planes[:, :v_planes], in_=by_plane[:, :v_planes])
+                if v_planes < Q:
+                    nc.scalar.copy(out=planes[:, v_planes:], in_=by_plane[:, v_planes:])
 
-            def split_input(name):
-                planes = prep.tile([P, BT, Q, FEAT], BF16, name="planes_" + name)
-                act_planes[name] = planes
-                by_plane = act_raw[name][:].rearrange("p t (n a) -> p t a n", a=Q)
-                nc.vector.tensor_copy(out=planes[:, 0], in_=by_plane[:, 0])
-                nc.scalar.copy(out=planes[:, 1, Q // 2 :], in_=by_plane[:, 1, Q // 2 :])
-                nc.vector.tensor_copy(out=planes[:, 1, : Q // 2], in_=by_plane[:, 1, : Q // 2])
-
-            def flip_input(name):
+            def flip_input(name, bt, v_banks):
                 plane_words = act_planes[name][:].bitcast(F32)
-                grouped = prep.tile([P, VERSIONS, BT, P, PACK], BF16, name="grouped_" + name, align_bytes=64)
-                grouped_words = grouped[:].bitcast(F32)
-                for bt in range(BT):
-                    for a0 in range(0, Q, 2):
-                        flipped = flip_pool.tile([P, BANK], F32, name="flipped", tag="flip")
-                        for a in range(2):
-                            for u in range(HALVES):
-                                block = HALVES * a + u
-                                nc.tensor.transpose(
-                                    flipped[:, block * P : (block + 1) * P],
-                                    plane_words[:, bt, a0 + a, u * P : (u + 1) * P],
-                                    ident[:],
-                                )
-                        copy = nc.scalar.copy if a0 == 0 else nc.vector.tensor_copy
-                        copy(
-                            out=grouped_words[:, a0 : a0 + 2, bt],
-                            in_=flipped[:].rearrange("p (a u b) -> p a b u", a=2, u=HALVES),
-                        )
-                codes = keep.tile([P, VERSIONS, BT, P], U32, name="codes_" + name, align_bytes=64)
-                scales = keep.tile([P, VERSIONS, BT, P], U8, name="scales_" + name, align_bytes=64)
-                act_grouped[name] = grouped
-                act_codes[name] = codes
-                act_scales[name] = scales
-                quantise_versions(name, 0, Q)
-                nc.vector.tensor_scalar_mul(
-                    out=grouped[:, Q:VERSIONS].rearrange("p s t b k -> p (s t b k)"),
-                    in0=grouped[:, 1:Q].rearrange("p s t b k -> p (s t b k)"),
-                    scalar1=-1.0,
-                )
+                if name not in act_grouped:
+                    act_grouped[name] = prep.tile(
+                        [P, VERSIONS, BT, P, PACK], BF16, name="grouped_" + name, align_bytes=64
+                    )
+                grouped_words = act_grouped[name][:].bitcast(F32)
+                for bank in range(2):
+                    flipped = flip_pool.tile([P, BANK], F32, name="flipped", tag="flip")
+                    for a in range(2):
+                        for u in range(HALVES):
+                            block = HALVES * a + u
+                            nc.tensor.transpose(
+                                flipped[:, block * P : (block + 1) * P],
+                                plane_words[:, bt, PLANES[2 * bank + a], u * P : (u + 1) * P],
+                                ident[:],
+                            )
+                    copy = nc.vector.tensor_copy if bank in v_banks else nc.scalar.copy
+                    to = slice(0, Q, Q - 1) if bank == 0 else slice(1, Q - 1)
+                    copy(
+                        out=grouped_words[:, to, bt],
+                        in_=flipped[:].rearrange("p (a u b) -> p a b u", a=2, u=HALVES),
+                    )
 
             def quantise_versions(name, first, count):
                 nc.vector.quantize_mx(
@@ -215,38 +247,56 @@ def tile_quaternionlstmcell_pa_kernel(
                     in_=act_grouped[name][:, first : first + count].rearrange("p s t b k -> p (s t b k)"),
                 )
 
+            def quantise_plain(name):
+                act_codes[name] = keep.tile([P, VERSIONS, BT, P], U32, name="codes_" + name, align_bytes=64)
+                act_scales[name] = keep.tile([P, VERSIONS, BT, P], U8, name="scales_" + name, align_bytes=64)
+                quantise_versions(name, 0, Q)
+
+            def negate(name):
+                grouped = act_grouped[name]
+                nc.vector.tensor_scalar_mul(
+                    out=grouped[:, Q:VERSIONS].rearrange("p s t b k -> p (s t b k)"),
+                    in0=grouped[:, 0 : Q - 1].rearrange("p s t b k -> p (s t b k)"),
+                    scalar1=-1.0,
+                )
+
             def quantise_negated(name):
                 quantise_versions(name, Q, 2)
                 quantise_versions(name, Q + 2, 1)
 
-            cand_acc = [new_acc() for d in range(Q)]
-
-            def candidate_quad(n):
-                for d in range(Q):
-                    multiply(cand_acc[d][:], d, 0, CAND * PARTS + n // UNIT, n % UNIT, whole)
-
-            first_round = [UNIT * u for u in range(PARTS)] + [UNIT * PARTS + g for g in range(n_units - PARTS)]
-
-            def prepare_ahead(n):
-                for u in range(n_units):
-                    if first_round[u] == n + LEAD:
-                        transpose_unit(u)
-                    if first_round[u] == n + 1:
-                        quantise_unit(u)
-
-            split_input("x")
-            flip_input("x")
-            for n in range(-LEAD, 0):
-                prepare_ahead(n)
+            split_input("x", 0, 2)
+            split_input("x", 1, 2)
+            flip_input("x", 0, (1,))
+            flip_input("x", 1, (1,))
+            quantise_plain("x")
+            negate("x")
+            transpose_unit(0)
+            quantise_unit(0)
             quantise_negated("x")
-            for n in range(UNIT * PARTS // 2):
-                prepare_ahead(n)
-                if n == 3:
-                    flip_input("h")
-                candidate_quad(n)
-                if n == 1:
-                    split_input("h")
+            transpose_unit(1)
+            first_tile(0, 0)
+            split_input("h", 0, 2)
+            split_input("h", 1, 2)
+            quantise_unit(1)
+            first_tile(1, 0)
+            flip_input("h", 0, (1,))
+            flip_input("h", 1, (1,))
+            transpose_unit(2)
+            first_tile(2, 0)
+            quantise_plain("h")
+            first_tile(3, 0)
+            quantise_unit(2)
+            negate("h")
             quantise_negated("h")
+            transpose_unit(3)
+            quantise_unit(3)
+            first_tile(0, 1)
+            transpose_unit(4)
+            first_tile(1, 1)
+            first_tile(2, 1)
+            transpose_unit(5)
+            quantise_unit(4)
+            first_tile(3, 1)
 
         cell_pool = stack.enter_context(tc.tile_pool(name="cell", bufs=BT))
 
@@ -254,139 +304,180 @@ def tile_quaternionlstmcell_pa_kernel(
             m0, width = cols
             return gate[:, m0 : m0 + width].unsqueeze(2).to_broadcast([P, width, Q])
 
-        open_gate = {}
+        whole = (0, OUT)
+        halves = ((0, OUT // 2), (OUT // 2, OUT // 2))
+        pieces = [(m0, CHUNK) for m0 in range(0, OUT, CHUNK)]
+        gates = {}
+        cell = {}
+        cand = cell_pool.tile([P, Q, OUT], F32, name="cand", tag="cand", bufs=1)
+        cand_pieces = {}
+        piece_acc = {}
+        fresh = [cell_pool.tile([P, OUT, Q], F32, name="fresh", tag="fresh") for bt in range(BT)]
+        squashed = [cell_pool.tile([P, OUT, Q], F32, name="squashed", tag="squashed") for bt in range(BT)]
 
-        def sigmoid_gate(stage):
-            gates[stage] = []
-            for bt in range(BT):
-                gate = cell_pool.tile([P, OUT], F32, name="gate%d" % stage, tag="gate%d" % stage)
-                nc.vector.tensor_tensor(out=gate[:], in0=open_gate[stage][bt][:], in1=bias[stage][:], op=ALU.add)
-                nc.scalar.activation(out=gate[:], in_=gate[:], func=ACT.Sigmoid)
-                gates[stage].append(gate)
+        def gate_sum(stage, bt):
+            gate = cell_pool.tile([P, OUT], F32, name="gate%d" % stage, tag="gate%d" % stage)
+            nc.vector.tensor_tensor(out=gate[:], in0=gate_accs[stage][bt][:], in1=bias[stage][:], op=ALU.add)
+            gates[stage, bt] = gate
 
-        def keep_old(bt, f_gate):
-            cell = cell_pool.tile([P, OUT, Q], F32, name="cell", tag="cell")
+        def gate_sigmoid(stage, bt):
+            gate = gates[stage, bt]
+            nc.scalar.activation(out=gate[:], in_=gate[:], func=ACT.Sigmoid)
+
+        def candidate_plane(d):
+            nc.vector.tensor_tensor(out=cand[:, d], in0=cand_acc[d][:], in1=bias[CAND][:, :, d], op=ALU.add)
+
+        def candidate_plane_tanh(d):
+            nc.scalar.activation(out=cand[:, d], in_=cand[:, d], func=ACT.Tanh)
+
+        def piece_passes(n):
+            acc = new_acc()
+            m0 = pieces[n][0]
+            u = first_unit[CAND, 0]
+            for d in range(Q):
+                for side in range(2):
+                    for comp in range(Q):
+                        first, last = side == 0 and comp == 0, side == 1 and comp == Q - 1
+                        of = u + (Q * side + comp) // UNIT
+                        multiply(
+                            acc[:, d * CHUNK : (d + 1) * CHUNK], d, 1, of, comp, first, last, slice(m0, m0 + CHUNK)
+                        )
+            piece_acc[n] = acc
+
+        def piece_sum(n):
+            m0 = pieces[n][0]
+            piece = cell_pool.tile([P, Q, CHUNK], F32, name="cand_piece", tag="cand_piece", bufs=4)
             nc.vector.tensor_tensor(
-                out=cell[:],
-                in0=over_components(f_gate, whole),
+                out=piece[:],
+                in0=piece_acc[n][:].rearrange("p (a m) -> p a m", a=Q),
+                in1=bias[CAND][:, m0 : m0 + CHUNK, :].rearrange("p m a -> p a m"),
+                op=ALU.add,
+            )
+            cand_pieces[n] = piece
+
+        def piece_tanh(n):
+            nc.scalar.activation(out=cand_pieces[n][:], in_=cand_pieces[n][:], func=ACT.Tanh)
+
+        def keep_old(bt):
+            cell[bt] = cell_pool.tile([P, OUT, Q], F32, name="cell", tag="cell")
+            nc.vector.tensor_tensor(
+                out=cell[bt][:],
+                in0=over_components(gates[F_GATE, bt], whole),
                 in1=c_raw[:, bt].rearrange("p (m a) -> p m a", a=Q),
                 op=ALU.mult,
             )
-            return cell
-
-        cand = cell_pool.tile([P, Q, OUT], F32, name="cand", tag="cand", bufs=1)
-        cand_pieces = []
-        fresh = [cell_pool.tile([P, OUT, Q], F32, name="fresh", tag="fresh") for bt in range(BT)]
-        squashed = [cell_pool.tile([P, OUT, Q], F32, name="squashed", tag="squashed") for bt in range(BT)]
-        cell = []
-        gates = {}
 
         def take_new(bt, cols, planes):
             m0, width = cols
             nc.vector.tensor_tensor(
                 out=fresh[bt][:, m0 : m0 + width],
-                in0=over_components(gates[I_GATE][bt], cols),
+                in0=over_components(gates[I_GATE, bt], cols),
                 in1=planes.rearrange("p a m -> p m a"),
                 op=ALU.mult,
             )
 
         def new_cell(bt, cols):
             m0, width = cols
-            part_of_cell = cell[bt][:, m0 : m0 + width]
-            nc.vector.tensor_tensor(out=part_of_cell, in0=part_of_cell, in1=fresh[bt][:, m0 : m0 + width], op=ALU.add)
-            nc.sync.dma_start(
-                out=c_rows[:, bt, m0 * Q : (m0 + width) * Q], in_=part_of_cell.rearrange("p m a -> p (m a)")
-            )
+            own = cell[bt][:, m0 : m0 + width]
+            nc.vector.tensor_tensor(out=own, in0=own, in1=fresh[bt][:, m0 : m0 + width], op=ALU.add)
+            nc.sync.dma_start(out=c_rows[:, bt, m0 * Q : (m0 + width) * Q], in_=own.rearrange("p m a -> p (m a)"))
 
         def squash(bt, cols):
             m0, width = cols
-            nc.scalar.activation(
-                out=squashed[bt][:, m0 : m0 + width], in_=cell[bt][:, m0 : m0 + width], func=ACT.Tanh
-            )
+            nc.scalar.activation(out=squashed[bt][:, m0 : m0 + width], in_=cell[bt][:, m0 : m0 + width], func=ACT.Tanh)
 
         def new_hidden(bt, cols):
             m0, width = cols
-            part_of_hidden = squashed[bt][:, m0 : m0 + width]
-            nc.vector.tensor_tensor(
-                out=part_of_hidden, in0=over_components(gates[O_GATE][bt], cols), in1=part_of_hidden, op=ALU.mult
-            )
-            nc.sync.dma_start(
-                out=h_rows[:, bt, m0 * Q : (m0 + width) * Q], in_=part_of_hidden.rearrange("p m a -> p (m a)")
-            )
+            own = squashed[bt][:, m0 : m0 + width]
+            nc.vector.tensor_tensor(out=own, in0=over_components(gates[O_GATE, bt], cols), in1=own, op=ALU.mult)
+            nc.sync.dma_start(out=h_rows[:, bt, m0 * Q : (m0 + width) * Q], in_=own.rearrange("p m a -> p (m a)"))
 
-        pieces = [(m0, CHUNK) for m0 in range(0, OUT, CHUNK)]
-
-        piece_acc = []
-
-        def piece_passes(n):
-            acc = new_acc()
-            for d in range(Q):
-                for part in range(PARTS):
-                    for comp in range(UNIT):
-                        multiply(acc[:, d * CHUNK : (d + 1) * CHUNK], d, 1, CAND * PARTS + part, comp, pieces[n])
-            piece_acc.append(acc)
-
-        def piece_candidate(n):
-            m0 = pieces[n][0]
-            acc = piece_acc[n]
-            piece = cell_pool.tile([P, Q, CHUNK], F32, name="cand_piece", tag="cand_piece")
-            nc.vector.tensor_tensor(
-                out=piece[:],
-                in0=acc[:].rearrange("p (a m) -> p a m", a=Q),
-                in1=bias[CAND][:, m0 : m0 + CHUNK, :].rearrange("p m a -> p a m"),
-                op=ALU.add,
-            )
-            nc.scalar.activation(out=piece[:], in_=piece[:], func=ACT.Tanh)
-            cand_pieces.append(piece)
-
-        for n in range(UNIT * PARTS // 2, UNIT * PARTS):
-            prepare_ahead(n)
-            candidate_quad(n)
-
-        def candidate_plane(d):
-            nc.vector.tensor_tensor(out=cand[:, d, :], in0=cand_acc[d][:], in1=bias[CAND][:, :, d], op=ALU.add)
-            nc.scalar.activation(out=cand[:, d, :], in_=cand[:, d, :], func=ACT.Tanh)
-
-        for d in range(BT):
-            candidate_plane(d)
-
-        for stage in (F_GATE, I_GATE, O_GATE):
-            accs = [new_acc() for bt in range(BT)]
-            for part in range(PARTS):
-                if stage == O_GATE and part == PARTS - 1:
-                    piece_passes(0)
-                prepare_ahead(first_round[stage * PARTS + part])
-                for comp in range(UNIT):
-                    for bt in range(BT):
-                        multiply(accs[bt][:], 0, bt, stage * PARTS + part, comp, whole)
-                if stage == F_GATE and part < Q - BT:
-                    candidate_plane(BT + part)
-                if stage == I_GATE and 1 <= part <= BT:
-                    cell.append(keep_old(part - 1, gates[F_GATE][part - 1]))
-                if stage == O_GATE and part == 1:
-                    take_new(0, whole, cand[:])
-                if stage == O_GATE and part == 2:
-                    new_cell(0, whole)
-                if stage == O_GATE and part == PARTS - 1:
-                    piece_candidate(0)
-                if part == 0 and stage > F_GATE:
-                    sigmoid_gate(stage - 1)
-            open_gate[stage] = accs
-        sigmoid_gate(O_GATE)
+        candidate_plane(0)
+        candidate_plane_tanh(0)
+        candidate_plane(1)
+        candidate_plane_tanh(1)
+        transpose_unit(6)
+        quantise_unit(5)
+        gate_unit(4)
+        candidate_plane(2)
+        candidate_plane_tanh(2)
+        transpose_unit(7)
+        quantise_unit(6)
+        gate_unit(5)
+        candidate_plane(3)
+        candidate_plane_tanh(3)
+        transpose_unit(8)
+        quantise_unit(7)
+        gate_unit(6)
+        transpose_unit(9)
+        quantise_unit(8)
+        gate_unit(7)
+        transpose_unit(10)
+        quantise_unit(9)
+        gate_unit(8)
+        gate_sum(F_GATE, 0)
+        gate_sigmoid(F_GATE, 0)
+        gate_sum(F_GATE, 1)
+        gate_sigmoid(F_GATE, 1)
+        transpose_unit(11)
+        quantise_unit(10)
+        gate_unit(9)
+        keep_old(0)
+        transpose_unit(12)
+        quantise_unit(11)
+        gate_unit(10)
+        keep_old(1)
+        transpose_unit(13)
+        quantise_unit(12)
+        gate_unit(11)
+        transpose_unit(14)
+        quantise_unit(13)
+        gate_unit(12)
+        gate_sum(I_GATE, 0)
+        gate_sigmoid(I_GATE, 0)
+        gate_sum(I_GATE, 1)
+        gate_sigmoid(I_GATE, 1)
+        transpose_unit(15)
+        quantise_unit(14)
+        gate_unit(13)
+        take_new(0, whole, cand[:])
+        quantise_unit(15)
+        gate_unit(14)
+        new_cell(0, whole)
+        piece_passes(0)
+        gate_unit(15)
+        piece_sum(0)
+        piece_tanh(0)
+        gate_sum(O_GATE, 0)
+        gate_sigmoid(O_GATE, 0)
+        gate_sum(O_GATE, 1)
+        gate_sigmoid(O_GATE, 1)
+        piece_passes(1)
+        take_new(1, pieces[0], cand_pieces[0][:])
+        piece_sum(1)
+        piece_tanh(1)
+        new_cell(1, pieces[0])
+        squash(1, pieces[0])
         squash(0, halves[0])
-
-        for n in range(len(pieces) + 2):
-            if 1 <= n < len(pieces):
-                piece_passes(n)
-            if 1 <= n <= len(pieces):
-                take_new(1, pieces[n - 1], cand_pieces[n - 1][:])
-                new_cell(1, pieces[n - 1])
-                squash(1, pieces[n - 1])
-            if 1 <= n < len(pieces):
-                piece_candidate(n)
-            if n >= 2:
-                new_hidden(1, pieces[n - 2])
-            if 1 <= n <= len(halves):
-                new_hidden(0, halves[n - 1])
-                if n < len(halves):
-                    squash(0, halves[n])
+        piece_passes(2)
+        take_new(1, pieces[1], cand_pieces[1][:])
+        piece_sum(2)
+        piece_tanh(2)
+        new_cell(1, pieces[1])
+        squash(1, pieces[1])
+        new_hidden(1, pieces[0])
+        new_hidden(0, halves[0])
+        piece_passes(3)
+        take_new(1, pieces[2], cand_pieces[2][:])
+        piece_sum(3)
+        piece_tanh(3)
+        squash(0, halves[1])
+        new_cell(1, pieces[2])
+        squash(1, pieces[2])
+        new_hidden(1, pieces[1])
+        take_new(1, pieces[3], cand_pieces[3][:])
+        new_cell(1, pieces[3])
+        squash(1, pieces[3])
+        new_hidden(0, halves[1])
+        new_hidden(1, pieces[2])
+        new_hidden(1, pieces[3])

@@ -39,7 +39,7 @@ FLOPS = 2 * BATCH * FEAT * OUT * 2 * (3 * Q + Q * Q)
 CAND, F_GATE, I_GATE, O_GATE = 0, 1, 2, 3
 GATES = (F_GATE, I_GATE, O_GATE)
 ORDER = ((CAND, 0), (F_GATE, 0), (I_GATE, 0), (O_GATE, 0))
-V_BANKS = {}
+V_BANKS = {6: (1,), 7: (1,), 8: (1,)}
 
 
 def input_version(d, w_comp):
@@ -346,11 +346,11 @@ def tile_quaternionlstmcell_pa_kernel(
 
         def piece_sum(n):
             m0 = pieces[n][0]
-            piece = cell_pool.tile([P, Q, CHUNK], F32, name="cand_piece", tag="cand_piece", bufs=4)
+            piece = cell_pool.tile([P, CHUNK, Q], F32, name="cand_piece", tag="cand_piece", bufs=4)
             nc.vector.tensor_tensor(
                 out=piece[:],
-                in0=piece_acc[n][:].rearrange("p (a m) -> p a m", a=Q),
-                in1=bias[CAND][:, m0 : m0 + CHUNK, :].rearrange("p m a -> p a m"),
+                in0=piece_acc[n][:].rearrange("p (a m) -> p m a", a=Q),
+                in1=bias[CAND][:, m0 : m0 + CHUNK, :],
                 op=ALU.add,
             )
             cand_pieces[n] = piece
@@ -367,13 +367,10 @@ def tile_quaternionlstmcell_pa_kernel(
                 op=ALU.mult,
             )
 
-        def take_new(bt, cols, planes):
+        def take_new(bt, cols, g):
             m0, width = cols
             nc.vector.tensor_tensor(
-                out=fresh[bt][:, m0 : m0 + width],
-                in0=over_components(gates[I_GATE, bt], cols),
-                in1=planes.rearrange("p a m -> p m a"),
-                op=ALU.mult,
+                out=fresh[bt][:, m0 : m0 + width], in0=over_components(gates[I_GATE, bt], cols), in1=g, op=ALU.mult
             )
 
         def new_cell(bt, cols):
@@ -396,51 +393,51 @@ def tile_quaternionlstmcell_pa_kernel(
         candidate_plane_tanh(0)
         candidate_plane(1)
         candidate_plane_tanh(1)
-        transpose_unit(6)
         quantise_unit(5)
+        transpose_unit(6)
         gate_unit(4)
         candidate_plane(2)
         candidate_plane_tanh(2)
-        transpose_unit(7)
         quantise_unit(6)
+        transpose_unit(7)
         gate_unit(5)
         candidate_plane(3)
         candidate_plane_tanh(3)
-        transpose_unit(8)
         quantise_unit(7)
+        transpose_unit(8)
         gate_unit(6)
-        transpose_unit(9)
         quantise_unit(8)
+        transpose_unit(9)
         gate_unit(7)
-        transpose_unit(10)
-        quantise_unit(9)
-        gate_unit(8)
         gate_sum(F_GATE, 0)
-        gate_sigmoid(F_GATE, 0)
         gate_sum(F_GATE, 1)
+        quantise_unit(9)
+        transpose_unit(10)
+        gate_sigmoid(F_GATE, 0)
         gate_sigmoid(F_GATE, 1)
-        transpose_unit(11)
+        gate_unit(8)
         quantise_unit(10)
+        transpose_unit(11)
         gate_unit(9)
         keep_old(0)
-        transpose_unit(12)
         quantise_unit(11)
+        transpose_unit(12)
         gate_unit(10)
         keep_old(1)
-        transpose_unit(13)
         quantise_unit(12)
+        transpose_unit(13)
         gate_unit(11)
-        transpose_unit(14)
         quantise_unit(13)
+        transpose_unit(14)
         gate_unit(12)
         gate_sum(I_GATE, 0)
         gate_sigmoid(I_GATE, 0)
         gate_sum(I_GATE, 1)
         gate_sigmoid(I_GATE, 1)
-        transpose_unit(15)
         quantise_unit(14)
+        transpose_unit(15)
         gate_unit(13)
-        take_new(0, whole, cand[:])
+        take_new(0, whole, cand[:].rearrange("p a m -> p m a"))
         quantise_unit(15)
         gate_unit(14)
         new_cell(0, whole)

@@ -81,6 +81,7 @@ def tile_quaternionlstmcell_pa_kernel(
         nc.scalar.activation(out=warm[:], in_=warm[:], func=ACT.Sigmoid)
 
         bias = {}
+        bias_col = []
         c_raw = keep.tile([P, BT, OUT * Q], BF16)
         act_raw = {}
         act_planes = {}
@@ -197,6 +198,9 @@ def tile_quaternionlstmcell_pa_kernel(
                         out=bias[CAND][:].rearrange("p m a -> p (m a)"),
                         in_=Uc_b.rearrange("m a -> (m a)").partition_broadcast(P),
                     )
+                if u == B_AT:
+                    bias_col.append(keep.tile([P, OUT // P, Q], BF16, name="bias_col"))
+                    nc.sync.dma_start(out=bias_col[0][:], in_=Uc_b.rearrange("(t p) a -> p t a", t=OUT // P))
                 if u == C_AT:
                     nc.sync.dma_start(out=c_raw[:], in_=c.rearrange("(p t) m a -> p t (m a)", t=BT))
                 w = weights[stage][side][c0 : c0 + UNIT]
@@ -312,7 +316,7 @@ def tile_quaternionlstmcell_pa_kernel(
         cand = cell_pool.tile([P, Q, OUT], F32, name="cand", tag="cand", bufs=1)
         cand_pieces = {}
         piece_acc = {}
-        fresh = [cell_pool.tile([P, OUT, Q], F32, name="fresh", tag="fresh") for bt in range(BT)]
+        fresh = [cell_pool.tile([P, OUT, Q], F32, name="fresh", tag="fresh", bufs=1)]
         squashed = [cell_pool.tile([P, OUT, Q], F32, name="squashed", tag="squashed") for bt in range(BT)]
 
         def gate_sum(stage, bt):
@@ -333,30 +337,69 @@ def tile_quaternionlstmcell_pa_kernel(
         def piece_passes(n):
             acc = new_acc()
             m0 = pieces[n][0]
-            u = first_unit[CAND, 0]
             for d in range(Q):
                 for side in range(2):
+                    name = ("x", "h")[side]
                     for comp in range(Q):
-                        first, last = side == 0 and comp == 0, side == 1 and comp == Q - 1
-                        of = u + (Q * side + comp) // UNIT
-                        multiply(
-                            acc[:, d * CHUNK : (d + 1) * CHUNK], d, 1, of, comp, first, last, slice(m0, m0 + CHUNK)
+                        u = first_unit[CAND, 0] + (Q * side + comp) // UNIT
+                        version = input_version(d, comp)
+                        nc.tensor.matmul_mx(
+                            out=acc[:, d * P : (d + 1) * P],
+                            lhsT=unit_codes[u][:, comp % UNIT, m0 : m0 + CHUNK].bitcast(FP8X4),
+                            lhsT_scale=unit_scales[u][:, comp % UNIT, m0 : m0 + CHUNK],
+                            rhs=act_codes[name][:, version, 1, :].bitcast(FP8X4),
+                            rhs_scale=act_scales[name][:, version, 1, :],
+                            start=(side == 0 and comp == 0),
+                            stop=(side == 1 and comp == Q - 1),
                         )
             piece_acc[n] = acc
 
-        def piece_sum(n):
-            m0 = pieces[n][0]
-            piece = cell_pool.tile([P, CHUNK, Q], F32, name="cand_piece", tag="cand_piece", bufs=4)
-            nc.vector.tensor_tensor(
-                out=piece[:],
-                in0=piece_acc[n][:].rearrange("p (a m) -> p m a", a=Q),
-                in1=bias[CAND][:, m0 : m0 + CHUNK, :],
-                op=ALU.add,
-            )
+        def piece_tanh(n):
+            piece = cell_pool.tile([P, Q, P], F32, name="cand_piece", tag="cand_piece", bufs=4)
+            for d in range(Q):
+                nc.scalar.activation(
+                    out=piece[:, d],
+                    in_=piece_acc[n][:, d * P : (d + 1) * P],
+                    func=ACT.Tanh,
+                    bias=bias_col[0][:, n, d : d + 1],
+                )
             cand_pieces[n] = piece
 
-        def piece_tanh(n):
-            nc.scalar.activation(out=cand_pieces[n][:], in_=cand_pieces[n][:], func=ACT.Tanh)
+        i_turned = []
+
+        def turn_gate():
+            bank = flip_pool.tile([P, BANK], F32, name="flipped", tag="flip")
+            for n in range(len(pieces)):
+                nc.tensor.transpose(
+                    bank[:, n * P : (n + 1) * P], gates[I_GATE, 1][:, n * CHUNK : (n + 1) * CHUNK], ident[:]
+                )
+            i_turned.append(bank)
+
+        def keep_turned():
+            turned_gate = cell_pool.tile([P, OUT], F32, name="turned_gate", tag="turned_gate", bufs=1)
+            nc.scalar.copy(out=turned_gate[:], in_=i_turned[0][:])
+            i_turned[0] = turned_gate
+
+        def piece_new(n):
+            g = cand_pieces[n]
+            gate = i_turned[0][:, n * P : (n + 1) * P].unsqueeze(1).to_broadcast([P, Q, P])
+            nc.vector.tensor_tensor(out=g[:], in0=gate, in1=g[:], op=ALU.mult)
+
+        turned = {}
+
+        def turn_piece(n):
+            bank = flip_pool.tile([P, BANK], F32, name="flipped", tag="flip")
+            for d in range(Q):
+                nc.tensor.transpose(bank[:, d * P : (d + 1) * P], cand_pieces[n][:, d], ident[:])
+            turned[n] = bank
+
+        def piece_cell(n):
+            m0, width = pieces[n]
+            own = cell[1][:, m0 : m0 + width]
+            nc.vector.tensor_tensor(
+                out=own, in0=own, in1=turned[n][:].rearrange("p (a m) -> p m a", a=Q), op=ALU.add
+            )
+            nc.sync.dma_start(out=c_rows[:, 1, m0 * Q : (m0 + width) * Q], in_=own.rearrange("p m a -> p (m a)"))
 
         def keep_old(bt):
             cell[bt] = cell_pool.tile([P, OUT, Q], F32, name="cell", tag="cell")
@@ -438,43 +481,45 @@ def tile_quaternionlstmcell_pa_kernel(
         transpose_unit(15)
         gate_unit(13)
         take_new(0, whole, cand[:].rearrange("p a m -> p m a"))
-        quantise_unit(15)
-        gate_unit(14)
-        new_cell(0, whole)
+        turn_gate()
+        keep_turned()
         piece_passes(0)
-        gate_unit(15)
-        piece_sum(0)
+        quantise_unit(15)
         piece_tanh(0)
-        gate_sum(O_GATE, 0)
-        gate_sigmoid(O_GATE, 0)
-        gate_sum(O_GATE, 1)
-        gate_sigmoid(O_GATE, 1)
         piece_passes(1)
-        take_new(1, pieces[0], cand_pieces[0][:])
-        piece_sum(1)
+        new_cell(0, whole)
+        gate_unit(14)
+        gate_unit(15)
+        piece_new(0)
         piece_tanh(1)
-        new_cell(1, pieces[0])
-        squash(1, pieces[0])
-        squash(0, halves[0])
+        piece_new(1)
+        gate_sum(O_GATE, 0)
+        gate_sum(O_GATE, 1)
+        gate_sigmoid(O_GATE, 0)
+        gate_sigmoid(O_GATE, 1)
+        turn_piece(0)
+        turn_piece(1)
         piece_passes(2)
-        take_new(1, pieces[1], cand_pieces[1][:])
-        piece_sum(2)
-        piece_tanh(2)
-        new_cell(1, pieces[1])
+        piece_cell(0)
+        squash(1, pieces[0])
+        piece_cell(1)
         squash(1, pieces[1])
+        piece_tanh(2)
+        squash(0, halves[0])
         new_hidden(1, pieces[0])
-        new_hidden(0, halves[0])
-        piece_passes(3)
-        take_new(1, pieces[2], cand_pieces[2][:])
-        piece_sum(3)
-        piece_tanh(3)
-        squash(0, halves[1])
-        new_cell(1, pieces[2])
-        squash(1, pieces[2])
+        piece_new(2)
         new_hidden(1, pieces[1])
-        take_new(1, pieces[3], cand_pieces[3][:])
-        new_cell(1, pieces[3])
+        piece_passes(3)
+        turn_piece(2)
+        new_hidden(0, halves[0])
+        piece_tanh(3)
+        piece_cell(2)
+        piece_new(3)
+        turn_piece(3)
+        squash(1, pieces[2])
+        squash(0, halves[1])
+        new_hidden(1, pieces[2])
+        piece_cell(3)
         squash(1, pieces[3])
         new_hidden(0, halves[1])
-        new_hidden(1, pieces[2])
         new_hidden(1, pieces[3])

from contextlib import ExitStack

import concourse.mybir as mybir
from concourse.masks import make_identity

F32 = mybir.dt.float32
BF16 = mybir.dt.bfloat16
U32 = mybir.dt.uint32
U8 = mybir.dt.uint8
FP8X4 = mybir.dt.float8_e4m3fn_x4
ACT = mybir.ActivationFunctionType
ALU = mybir.AluOpType

P = 128
PACK = 4
BATCH, FEAT, OUT, Q = 256, 512, 512, 4
BT = BATCH // P
WORDS = FEAT // 2
HALVES = WORDS // P
BANK = 512
CHUNK = BANK // Q
PLANES = (1, 0, 2, 3)
COLS = BANK // BT
PARTS = OUT // COLS
UNIT = 2
SPAN = P // UNIT
ROWS = OUT // SPAN
VERSIONS = 2 * Q - 1

HAM = (
    ((0, 1.0), (1, 1.0), (2, 1.0), (3, 1.0)),
    ((1, -1.0), (0, 1.0), (3, 1.0), (2, -1.0)),
    ((2, -1.0), (3, -1.0), (0, 1.0), (1, 1.0)),
    ((3, -1.0), (2, 1.0), (1, -1.0), (0, 1.0)),
)

FLOPS = 2 * BATCH * FEAT * OUT * 2 * (3 * Q + Q * Q)

CAND, F_GATE, I_GATE, O_GATE = 0, 1, 2, 3
GATES = (F_GATE, I_GATE, O_GATE)
ORDER = ((CAND, 0), (F_GATE, 0), (I_GATE, 0), (O_GATE, 0))
V_BANKS = {6: (1,), 7: (1,), 8: (1,)}


def input_version(d, w_comp):
    a = [a for a in range(Q) if HAM[a][d][0] == w_comp][0]
    if a == 0:
        return Q - 1
    return a - 1 if HAM[a][d][1] > 0 else Q - 1 + a


def tile_quaternionlstmcell_pa_kernel(
    tc, x, h, c, Wi_w, Wf_w, Wo_w, Wc_w, Ui_w, Uf_w, Uo_w, Uc_w, Ui_br, Uf_br, Uo_br, Uc_b, out_0, out_1
):
    nc = tc.nc
    weights = {CAND: (Wc_w, Uc_w), F_GATE: (Wf_w, Uf_w), I_GATE: (Wi_w, Ui_w), O_GATE: (Wo_w, Uo_w)}
    gate_bias = {F_GATE: Uf_br, I_GATE: Ui_br, O_GATE: Uo_br}
    units = []
    for stage, part in ORDER:
        units += [(stage, side, c0, UNIT, 0, OUT) for side in range(2) for c0 in range(0, Q, UNIT)]
    first_unit = {}
    for u in range(len(units)):
        first_unit.setdefault((units[u][0], units[u][4] // COLS), u)
    h_rows = out_0.rearrange("(p t) m a -> p t (m a)", t=BT)
    c_rows = out_1.rearrange("(p t) m a -> p t (m a)", t=BT)

    with ExitStack() as stack:
        stack.enter_context(tc.manual_schedule())
        keep = stack.enter_context(tc.tile_pool(name="keep", bufs=1))
        raw_pool = stack.enter_context(tc.tile_pool(name="raw", bufs=7))
        grouped_pool = stack.enter_context(tc.tile_pool(name="grouped", bufs=3))
        cand_code_pool = stack.enter_context(tc.tile_pool(name="cand_codes", bufs=4))
        code_pool = stack.enter_context(tc.tile_pool(name="codes", bufs=4))
        flip_pool = stack.enter_context(tc.psum_pool(name="flip", bufs=4))
        acc_pool = stack.enter_context(tc.psum_pool(name="acc", bufs=4))

        ident = keep.tile([P, P], F32)
        make_identity(nc, ident[:])
        warm = keep.tile([P, 1], F32)
        nc.vector.memset(warm[:], 0.0)
        nc.scalar.activation(out=warm[:], in_=warm[:], func=ACT.Sigmoid)

        bias = {}
        bias_col = []
        c_raw = keep.tile([P, BT, OUT * Q], BF16)
        act_raw = {}
        act_planes = {}
        act_grouped = {}
        act_codes = {}
        act_scales = {}
        raw_units = []
        grouped_units = {}
        unit_codes = {}
        unit_scales = {}

        def transpose_unit(u):
            raw_words = raw_units[u][:].bitcast(F32)
            grouped = grouped_pool.tile([P, UNIT, OUT, PACK], BF16, name="grouped_unit", tag="grouped_unit", align_bytes=64)
            grouped_words = grouped[:].rearrange("p c m k -> p (c m) k").bitcast(F32)
            for g in range(ROWS // 2):
                flipped = flip_pool.tile([P, BANK], F32, name="flipped", tag="flip")
                for j in range(2):
                    for u2 in range(HALVES):
                        block = HALVES * j + u2
                        nc.tensor.transpose(
                            flipped[:, block * P : (block + 1) * P],
                            raw_words[:, 2 * g + j, u2 * P : (u2 + 1) * P],
                            ident[:],
                        )
                copy = nc.vector.tensor_copy if g in V_BANKS.get(u, ()) else nc.scalar.copy
                copy(
                    out=grouped_words.rearrange("p (q g j) u -> p g q j u", g=ROWS // 2, j=2)[:, g],
                    in_=flipped[:].rearrange("p (j u q) -> p q j u", j=2, u=HALVES),
                )
            grouped_units[u] = grouped

        def quantise_unit(u):
            pool = cand_code_pool if units[u][0] == CAND else code_pool
            codes = pool.tile([P, UNIT, OUT], U32, name="unit_codes", tag="unit_codes", align_bytes=64)
            scales = pool.tile([P, UNIT, OUT], U8, name="unit_scales", tag="unit_scales", align_bytes=64)
            nc.vector.quantize_mx(
                out=codes[:].rearrange("p c m -> p (c m)").bitcast(FP8X4),
                scales=scales[:].rearrange("p c m -> p (c m)"),
                in_=grouped_units[u][:].rearrange("p c m k -> p (c m k)"),
            )
            unit_codes[u] = codes
            unit_scales[u] = scales

        def multiply(acc, d, bt, u, comp, start, stop, cols=slice(0, OUT)):
            side, c0 = units[u][1:3]
            name = ("x", "h")[side]
            version = input_version(d, comp)
            nc.tensor.matmul_mx(
                out=acc,
                lhsT=act_codes[name][:, version, bt, :].bitcast(FP8X4),
                lhsT_scale=act_scales[name][:, version, bt, :],
                rhs=unit_codes[u][:, comp - c0, cols].bitcast(FP8X4),
                rhs_scale=unit_scales[u][:, comp - c0, cols],
                start=start,
                stop=stop,
            )

        def new_acc():
            acc = acc_pool.tile([P, BANK], F32, name="acc", tag="acc")
            return acc

        def group(stage, acc, half, d, bt, part):
            u = first_unit[stage, 0]
            for side in range(2):
                for comp in range(Q):
                    first, last = side == 0 and comp == 0, side == 1 and comp == Q - 1
                    of = u + (Q * side + comp) // UNIT
                    multiply(acc[:, COLS * half : COLS * (half + 1)], d, bt, of, comp, first, last, columns(part))

        def columns(part):
            return slice(COLS * part, COLS * (part + 1))

        cand_acc = []

        def first_tile(comp, side):
            if not cand_acc:
                cand_acc.extend([new_acc() for d in range(Q)])
            for d in range(Q):
                first, last = side == 0 and comp == 0, side == 1 and comp == Q - 1
                multiply(cand_acc[d][:], d, 0, first_unit[CAND, 0] + (Q * side + comp) // UNIT, comp, first, last)

        gate_accs = {}

        def gate_unit(u):
            stage, side, c0 = units[u][:3]
            if stage not in gate_accs:
                gate_accs[stage] = [new_acc() for bt in range(BT)]
            for comp in (c0, c0 + 1):
                for bt in range(BT):
                    first, last = side == 0 and comp == 0, side == 1 and comp == Q - 1
                    multiply(gate_accs[stage][bt][:], 0, bt, u, comp, first, last)

        with tc.tile_pool(name="prep", bufs=1) as prep:
            def load_input(name, v):
                act_raw[name] = prep.tile([P, BT, FEAT * Q], BF16, name="raw_" + name)
                rows = v.rearrange("(p t) n a -> p t (n a)", t=BT)
                for bt in range(BT):
                    nc.sync.dma_start(out=act_raw[name][:, bt], in_=rows[:, bt])

            X_AT, H_AT, BF_AT, B2_AT, C_AT, B_AT = 0, 2, 9, 5, 11, 9
            for u in range(len(units)):
                if u == X_AT:
                    load_input("x", x)
                stage, side, c0, comps, m0, cols = units[u]
                if u == H_AT:
                    load_input("h", h)
                for g in ((F_GATE,) if u == BF_AT else ()) + ((I_GATE, O_GATE) if u == B_AT else ()):
                    bias[g] = keep.tile([P, OUT], BF16, name="bias_gate%d" % g)
                    nc.sync.dma_start(out=bias[g][:], in_=gate_bias[g].partition_broadcast(P))
                if u == B2_AT:
                    bias[CAND] = keep.tile([P, OUT, Q], BF16, name="bias_cand")
                    nc.sync.dma_start(
                        out=bias[CAND][:].rearrange("p m a -> p (m a)"),
                        in_=Uc_b.rearrange("m a -> (m a)").partition_broadcast(P),
                    )
                if u == B_AT:
                    bias_col.append(keep.tile([P, OUT // P, Q], BF16, name="bias_col"))
                    nc.sync.dma_start(out=bias_col[0][:], in_=Uc_b.rearrange("(t p) a -> p t a", t=OUT // P))
                if u == C_AT:
                    nc.sync.dma_start(out=c_raw[:], in_=c.rearrange("(p t) m a -> p t (m a)", t=BT))
                w = weights[stage][side][c0 : c0 + UNIT]
                raw = raw_pool.tile([P, ROWS, FEAT], BF16, name="raw_unit", tag="raw_unit")
                nc.sync.dma_start(
                    out=raw[:].rearrange("q j n -> q (j n)"), in_=w.rearrange("c (p j) n -> (c p) (j n)", j=ROWS)
                )
                raw_units.append(raw)

            def split_input(name, bt, v_planes):
                if name not in act_planes:
                    act_planes[name] = prep.tile([P, BT, Q, FEAT], BF16, name="planes_" + name)
                planes = act_planes[name][:, bt]
                by_plane = act_raw[name][:, bt].rearrange("p (n a) -> p a n", a=Q)
                if v_planes > 0:
                    nc.vector.tensor_copy(out=planes[:, :v_planes], in_=by_plane[:, :v_planes])
                if v_planes < Q:
                    nc.scalar.copy(out=planes[:, v_planes:], in_=by_plane[:, v_planes:])

            def flip_input(name, bt, v_banks):
                plane_words = act_planes[name][:].bitcast(F32)
                if name not in act_grouped:
                    act_grouped[name] = prep.tile(
                        [P, VERSIONS, BT, P, PACK], BF16, name="grouped_" + name, align_bytes=64
                    )
                grouped_words = act_grouped[name][:].bitcast(F32)
                for bank in range(2):
                    flipped = flip_pool.tile([P, BANK], F32, name="flipped", tag="flip")
                    for a in range(2):
                        for u in range(HALVES):
                            block = HALVES * a + u
                            nc.tensor.transpose(
                                flipped[:, block * P : (block + 1) * P],
                                plane_words[:, bt, PLANES[2 * bank + a], u * P : (u + 1) * P],
                                ident[:],
                            )
                    copy = nc.vector.tensor_copy if bank in v_banks else nc.scalar.copy
                    to = slice(0, Q, Q - 1) if bank == 0 else slice(1, Q - 1)
                    copy(
                        out=grouped_words[:, to, bt],
                        in_=flipped[:].rearrange("p (a u b) -> p a b u", a=2, u=HALVES),
                    )

            def quantise_versions(name, first, count):
                nc.vector.quantize_mx(
                    out=act_codes[name][:, first : first + count].rearrange("p s t b -> p (s t b)").bitcast(FP8X4),
                    scales=act_scales[name][:, first : first + count].rearrange("p s t b -> p (s t b)"),
                    in_=act_grouped[name][:, first : first + count].rearrange("p s t b k -> p (s t b k)"),
                )

            def quantise_plain(name):
                act_codes[name] = keep.tile([P, VERSIONS, BT, P], U32, name="codes_" + name, align_bytes=64)
                act_scales[name] = keep.tile([P, VERSIONS, BT, P], U8, name="scales_" + name, align_bytes=64)
                quantise_versions(name, 0, Q)

            def negate(name):
                grouped = act_grouped[name]
                nc.vector.tensor_scalar_mul(
                    out=grouped[:, Q:VERSIONS].rearrange("p s t b k -> p (s t b k)"),
                    in0=grouped[:, 0 : Q - 1].rearrange("p s t b k -> p (s t b k)"),
                    scalar1=-1.0,
                )

            def quantise_negated(name):
                quantise_versions(name, Q, 2)
                quantise_versions(name, Q + 2, 1)

            split_input("x", 0, 2)
            split_input("x", 1, 2)
            flip_input("x", 0, (1,))
            flip_input("x", 1, (1,))
            quantise_plain("x")
            negate("x")
            transpose_unit(0)
            quantise_unit(0)
            quantise_negated("x")
            transpose_unit(1)
            first_tile(0, 0)
            split_input("h", 0, 2)
            split_input("h", 1, 2)
            quantise_unit(1)
            first_tile(1, 0)
            flip_input("h", 0, (1,))
            flip_input("h", 1, (1,))
            transpose_unit(2)
            first_tile(2, 0)
            quantise_plain("h")
            first_tile(3, 0)
            quantise_unit(2)
            negate("h")
            quantise_negated("h")
            transpose_unit(3)
            quantise_unit(3)
            first_tile(0, 1)
            transpose_unit(4)
            first_tile(1, 1)
            first_tile(2, 1)
            transpose_unit(5)
            quantise_unit(4)
            first_tile(3, 1)

        cell_pool = stack.enter_context(tc.tile_pool(name="cell", bufs=BT))

        def over_components(gate, cols):
            m0, width = cols
            return gate[:, m0 : m0 + width].unsqueeze(2).to_broadcast([P, width, Q])

        whole = (0, OUT)
        halves = ((0, OUT // 2), (OUT // 2, OUT // 2))
        pieces = [(m0, CHUNK) for m0 in range(0, OUT, CHUNK)]
        gates = {}
        cell = {}
        cand = cell_pool.tile([P, Q, OUT], F32, name="cand", tag="cand", bufs=1)
        cand_pieces = {}
        piece_acc = {}
        fresh = [cell_pool.tile([P, OUT, Q], F32, name="fresh", tag="fresh", bufs=1)]
        squashed = [cell_pool.tile([P, OUT, Q], F32, name="squashed", tag="squashed") for bt in range(BT)]

        def gate_sum(stage, bt):
            gate = cell_pool.tile([P, OUT], F32, name="gate%d" % stage, tag="gate%d" % stage)
            nc.vector.tensor_tensor(out=gate[:], in0=gate_accs[stage][bt][:], in1=bias[stage][:], op=ALU.add)
            gates[stage, bt] = gate

        def gate_sigmoid(stage, bt):
            gate = gates[stage, bt]
            nc.scalar.activation(out=gate[:], in_=gate[:], func=ACT.Sigmoid)

        def candidate_plane(d):
            nc.vector.tensor_tensor(out=cand[:, d], in0=cand_acc[d][:], in1=bias[CAND][:, :, d], op=ALU.add)

        def candidate_plane_tanh(d):
            nc.scalar.activation(out=cand[:, d], in_=cand[:, d], func=ACT.Tanh)

        def piece_passes(n):
            acc = new_acc()
            m0 = pieces[n][0]
            for d in range(Q):
                for side in range(2):
                    name = ("x", "h")[side]
                    for comp in range(Q):
                        u = first_unit[CAND, 0] + (Q * side + comp) // UNIT
                        version = input_version(d, comp)
                        nc.tensor.matmul_mx(
                            out=acc[:, d * P : (d + 1) * P],
                            lhsT=unit_codes[u][:, comp % UNIT, m0 : m0 + CHUNK].bitcast(FP8X4),
                            lhsT_scale=unit_scales[u][:, comp % UNIT, m0 : m0 + CHUNK],
                            rhs=act_codes[name][:, version, 1, :].bitcast(FP8X4),
                            rhs_scale=act_scales[name][:, version, 1, :],
                            start=(side == 0 and comp == 0),
                            stop=(side == 1 and comp == Q - 1),
                        )
            piece_acc[n] = acc

        def piece_tanh(n):
            piece = cell_pool.tile([P, Q, P], F32, name="cand_piece", tag="cand_piece", bufs=4)
            for d in range(Q):
                nc.scalar.activation(
                    out=piece[:, d],
                    in_=piece_acc[n][:, d * P : (d + 1) * P],
                    func=ACT.Tanh,
                    bias=bias_col[0][:, n, d : d + 1],
                )
            cand_pieces[n] = piece

        i_turned = []

        def turn_gate():
            bank = flip_pool.tile([P, BANK], F32, name="flipped", tag="flip")
            for n in range(len(pieces)):
                nc.tensor.transpose(
                    bank[:, n * P : (n + 1) * P], gates[I_GATE, 1][:, n * CHUNK : (n + 1) * CHUNK], ident[:]
                )
            i_turned.append(bank)

        def keep_turned():
            turned_gate = cell_pool.tile([P, OUT], F32, name="turned_gate", tag="turned_gate", bufs=1)
            nc.scalar.copy(out=turned_gate[:], in_=i_turned[0][:])
            i_turned[0] = turned_gate

        def piece_new(n):
            g = cand_pieces[n]
            gate = i_turned[0][:, n * P : (n + 1) * P].unsqueeze(1).to_broadcast([P, Q, P])
            nc.vector.tensor_tensor(out=g[:], in0=gate, in1=g[:], op=ALU.mult)

        turned = {}

        def turn_piece(n):
            bank = flip_pool.tile([P, BANK], F32, name="flipped", tag="flip")
            for d in range(Q):
                nc.tensor.transpose(bank[:, d * P : (d + 1) * P], cand_pieces[n][:, d], ident[:])
            turned[n] = bank

        def piece_cell(n):
            m0, width = pieces[n]
            own = cell[1][:, m0 : m0 + width]
            nc.vector.tensor_tensor(
                out=own, in0=own, in1=turned[n][:].rearrange("p (a m) -> p m a", a=Q), op=ALU.add
            )
            nc.sync.dma_start(out=c_rows[:, 1, m0 * Q : (m0 + width) * Q], in_=own.rearrange("p m a -> p (m a)"))

        def keep_old(bt):
            cell[bt] = cell_pool.tile([P, OUT, Q], F32, name="cell", tag="cell")
            nc.vector.tensor_tensor(
                out=cell[bt][:],
                in0=over_components(gates[F_GATE, bt], whole),
                in1=c_raw[:, bt].rearrange("p (m a) -> p m a", a=Q),
                op=ALU.mult,
            )

        def take_new(bt, cols, g):
            m0, width = cols
            nc.vector.tensor_tensor(
                out=fresh[bt][:, m0 : m0 + width], in0=over_components(gates[I_GATE, bt], cols), in1=g, op=ALU.mult
            )

        def new_cell(bt, cols):
            m0, width = cols
            own = cell[bt][:, m0 : m0 + width]
            nc.vector.tensor_tensor(out=own, in0=own, in1=fresh[bt][:, m0 : m0 + width], op=ALU.add)
            nc.sync.dma_start(out=c_rows[:, bt, m0 * Q : (m0 + width) * Q], in_=own.rearrange("p m a -> p (m a)"))

        def squash(bt, cols):
            m0, width = cols
            nc.scalar.activation(out=squashed[bt][:, m0 : m0 + width], in_=cell[bt][:, m0 : m0 + width], func=ACT.Tanh)

        def new_hidden(bt, cols):
            m0, width = cols
            own = squashed[bt][:, m0 : m0 + width]
            nc.vector.tensor_tensor(out=own, in0=over_components(gates[O_GATE, bt], cols), in1=own, op=ALU.mult)
            nc.sync.dma_start(out=h_rows[:, bt, m0 * Q : (m0 + width) * Q], in_=own.rearrange("p m a -> p (m a)"))

        candidate_plane(0)
        candidate_plane_tanh(0)
        candidate_plane(1)
        candidate_plane_tanh(1)
        quantise_unit(5)
        transpose_unit(6)
        gate_unit(4)
        candidate_plane(2)
        candidate_plane_tanh(2)
        quantise_unit(6)
        transpose_unit(7)
        gate_unit(5)
        candidate_plane(3)
        candidate_plane_tanh(3)
        quantise_unit(7)
        transpose_unit(8)
        gate_unit(6)
        quantise_unit(8)
        transpose_unit(9)
        gate_unit(7)
        gate_sum(F_GATE, 0)
        gate_sum(F_GATE, 1)
        quantise_unit(9)
        transpose_unit(10)
        gate_sigmoid(F_GATE, 0)
        gate_sigmoid(F_GATE, 1)
        gate_unit(8)
        quantise_unit(10)
        transpose_unit(11)
        gate_unit(9)
        keep_old(0)
        quantise_unit(11)
        transpose_unit(12)
        gate_unit(10)
        keep_old(1)
        quantise_unit(12)
        transpose_unit(13)
        gate_unit(11)
        quantise_unit(13)
        transpose_unit(14)
        gate_unit(12)
        gate_sum(I_GATE, 0)
        gate_sigmoid(I_GATE, 0)
        gate_sum(I_GATE, 1)
        gate_sigmoid(I_GATE, 1)
        quantise_unit(14)
        transpose_unit(15)
        gate_unit(13)
        take_new(0, whole, cand[:].rearrange("p a m -> p m a"))
        turn_gate()
        keep_turned()
        piece_passes(0)
        quantise_unit(15)
        piece_tanh(0)
        piece_passes(1)
        new_cell(0, whole)
        gate_unit(14)
        gate_unit(15)
        piece_new(0)
        piece_tanh(1)
        piece_new(1)
        gate_sum(O_GATE, 0)
        gate_sum(O_GATE, 1)
        gate_sigmoid(O_GATE, 0)
        gate_sigmoid(O_GATE, 1)
        turn_piece(0)
        turn_piece(1)
        piece_passes(2)
        piece_cell(0)
        squash(1, pieces[0])
        piece_cell(1)
        squash(1, pieces[1])
        piece_tanh(2)
        squash(0, halves[0])
        new_hidden(1, pieces[0])
        piece_new(2)
        new_hidden(1, pieces[1])
        piece_passes(3)
        turn_piece(2)
        new_hidden(0, halves[0])
        piece_tanh(3)
        piece_cell(2)
        piece_new(3)
        turn_piece(3)
        squash(1, pieces[2])
        squash(0, halves[1])
        new_hidden(1, pieces[2])
        piece_cell(3)
        squash(1, pieces[3])
        new_hidden(0, halves[1])
        new_hidden(1, pieces[3])
